import numpy as np
import ml_dtypes


def mxq(x, axis, fmt="e4m3"):
    dtype, down = {"e4m3": (ml_dtypes.float8_e4m3fn, 7), "e5m2": (ml_dtypes.float8_e5m2, 14)}[fmt]
    v = np.moveaxis(np.asarray(x, np.float32).astype(ml_dtypes.bfloat16).astype(np.float64), axis, -1)
    blocks = v.reshape(v.shape[:-1] + (-1, 32))
    amax = np.abs(blocks).max(-1, keepdims=True)
    byte = np.maximum(np.where(amax > 0, np.frexp(amax)[1] - 1 + 127, 0) - down, 1)
    scale = np.exp2(byte - 127.0)
    codes = (blocks / scale).astype(np.float32).astype(dtype).astype(np.float64)
    return np.moveaxis((codes * scale).reshape(v.shape), -1, axis)


WIDE = False


def mx_kscale(k):
    if not WIDE:
        return np.ones(k)
    levels = np.array([10, -10, 5, -5, 0])
    a = np.random.permutation(np.resize(levels, k // 512 * 4)).reshape(k // 512, 4)
    idx = np.arange(k)
    return np.exp2(a[idx // 512, idx % 128 // 32])


BF16 = ml_dtypes.bfloat16


def bf(x):
    return np.asarray(x, np.float32).astype(BF16)


def f64(x):
    return np.asarray(x).astype(np.float64)


E2M1 = np.array([0.0, 0.5, 1.0, 1.5, 2.0, 3.0, 4.0, 6.0, -0.0, -0.5, -1.0, -1.5, -2.0, -3.0, -4.0, -6.0])


def pack_weight(w, fmt):
    k, n = w.shape
    w = f64(bf(w)).reshape(k // 32, 32, n)
    amax = np.abs(w).max(1)
    if fmt == "e4m3":
        byte = np.frexp(amax)[1] - 1 + 127 - 7
    else:
        mant, ex = np.frexp(amax / 6.0)
        byte = np.where(mant > 0.5, ex, ex - 1) + 127
    byte = np.clip(np.where(amax > 0, byte, 1), 1, 254)
    scaled = (w * np.exp2(127.0 - byte)[:, None, :]).reshape(k, n).astype(np.float32)
    by_word = np.ascontiguousarray(scaled.reshape(k // 512, 128, 4, n).transpose(0, 1, 3, 2))
    if fmt == "e4m3":
        words = by_word.astype(ml_dtypes.float8_e4m3fn).view(np.uint8)
    else:
        c = by_word.astype(ml_dtypes.float4_e2m1fn).view(np.uint8) & 0xF
        words = c[..., 0::2] | (c[..., 1::2] << 4)
    return np.ascontiguousarray(words), np.ascontiguousarray(byte.astype(np.uint8).reshape(k // 512, 16, n))


def unpack_weight(words, scales, fmt):
    g, p, n, _ = words.shape
    if fmt == "e4m3":
        vals = np.ascontiguousarray(words).view(ml_dtypes.float8_e4m3fn).astype(np.float64)
    else:
        nib = np.empty((g, p, n, 4), np.uint8)
        nib[..., 0::2] = words & 0xF
        nib[..., 1::2] = words >> 4
        vals = E2M1[nib]
    vals = vals * np.repeat(np.exp2(scales.astype(np.float64) - 127.0), 8, axis=1)[..., None]
    return vals.transpose(0, 1, 3, 2).reshape(g * 512, n)


B, D_IN, D_OUT = 4096, 1024, 256
FMT = "e4m3"


def sigmoid(v):
    return 1.0 / (1.0 + np.exp(-v))


def setup_inputs():
    s = mx_kscale(D_IN)
    w = lambda: pack_weight(np.random.standard_normal((D_IN, D_OUT)) / np.sqrt(D_IN) / s[:, None], FMT)
    b = lambda: bf(np.random.standard_normal(D_OUT) * 0.5)
    x = bf(np.random.standard_normal((B, D_IN)) * s)
    Wxi_words, Wxi_scales = w()
    bxi = b()
    Wxc_words, Wxc_scales = w()
    bxc = b()
    Wxo_words, Wxo_scales = w()
    bxo = b()
    return {"x": x,
            "Wxi_words": Wxi_words, "Wxi_scales": Wxi_scales, "bxi": bxi,
            "Wxc_words": Wxc_words, "Wxc_scales": Wxc_scales, "bxc": bxc,
            "Wxo_words": Wxo_words, "Wxo_scales": Wxo_scales, "bxo": bxo}


def reference(x, Wxi_words, Wxi_scales, bxi, Wxc_words, Wxc_scales, bxc, Wxo_words, Wxo_scales, bxo):
    xq = mxq(f64(x), 1, "e4m3")
    gi = (xq @ unpack_weight(Wxi_words, Wxi_scales, FMT)) + f64(bxi)
    gc = (xq @ unpack_weight(Wxc_words, Wxc_scales, FMT)) + f64(bxc)
    go = (xq @ unpack_weight(Wxo_words, Wxo_scales, FMT)) + f64(bxo)
    i = sigmoid(gi)
    c = np.tanh(gc)
    o = sigmoid(go)
    new_state = c * i
    return np.tanh(new_state) * o

@@ -1,0 +1,210 @@
+from contextlib import ExitStack
+
+import concourse.mybir as mybir
+from concourse.masks import make_identity
+
+F32 = mybir.dt.float32
+BF16 = mybir.dt.bfloat16
+I32 = mybir.dt.int32
+U32 = mybir.dt.uint32
+U8 = mybir.dt.uint8
+FP8X4 = mybir.dt.float8_e4m3fn_x4
+FUNC = mybir.ActivationFunctionType
+
+P = 128
+PACK = 4
+K_PASS = P * PACK
+BATCH, D_IN, D_OUT = 4096, 1024, 256
+PASSES = D_IN // K_PASS
+GATES = 3
+HALVES = D_OUT // P
+CHUNK = 512
+ROWS = CHUNK // P
+N_CHUNKS = BATCH // CHUNK
+WORDS = K_PASS // 2
+
+FLOPS = 2 * BATCH * D_IN * GATES * D_OUT
+
+
+def tile_lstm_pa_t_kernel(
+    tc, x, Wxi_words, Wxi_scales, bxi, Wxc_words, Wxc_scales, bxc, Wxo_words, Wxo_scales, bxo, out
+):
+    nc = tc.nc
+    gate_words = [Wxi_words, Wxc_words, Wxo_words]
+    gate_scales = [Wxi_scales, Wxc_scales, Wxo_scales]
+    gate_biases = [bxi, bxc, bxo]
+    gate_funcs = [FUNC.Sigmoid, FUNC.Tanh, FUNC.Sigmoid]
+
+    x_view = x.rearrange("(c p j) k -> c p j k", p=P, j=ROWS)
+    out_view = out.rearrange("(c p j) f -> c p j f", p=P, j=ROWS)
+
+    with ExitStack() as stack:
+        consts = stack.enter_context(tc.tile_pool(name="consts", bufs=1))
+        x_pool = stack.enter_context(tc.tile_pool(name="x", bufs=N_CHUNKS))
+        grouped_pool = stack.enter_context(tc.tile_pool(name="grouped", bufs=4))
+        operand_pool = stack.enter_context(tc.tile_pool(name="operand", bufs=4))
+        gate_pool = stack.enter_context(tc.tile_pool(name="gate", bufs=3))
+        out_pool = stack.enter_context(tc.tile_pool(name="out", bufs=3))
+        banks = stack.enter_context(tc.psum_pool(name="banks", bufs=8))
+        stack.enter_context(tc.manual_schedule())
+
+        x_tiles, grouped_tiles, code_tiles, plane_tiles = {}, {}, {}, {}
+        gate_tiles, state_tiles, tanh_tiles, result_tiles = {}, {}, {}, {}
+
+        ident = consts.tile([P, P], F32)
+        make_identity(nc, ident[:])
+
+        bias_rows = consts.tile([P, P], BF16)
+        nc.vector.memset(bias_rows[:], 0.0)
+        for gate in range(GATES):
+            nc.scalar.dma_start(
+                out=bias_rows[HALVES * gate : HALVES * (gate + 1), :],
+                in_=gate_biases[gate].rearrange("(h f) -> h f", h=HALVES),
+            )
+
+        bias_rows_f32 = consts.tile([P, P], F32)
+        nc.gpsimd.tensor_copy(out=bias_rows_f32[:], in_=bias_rows[:])
+
+        warm = consts.tile([P, 2], F32)
+        nc.vector.memset(warm[:], 0.0)
+        nc.scalar.activation(out=warm[:, 1:2], in_=warm[:, 0:1], func=FUNC.Sigmoid)
+
+        def load_chunk(c):
+            x_sb = x_pool.tile([P, ROWS, D_IN], BF16)
+            for half in range(2):
+                js = slice(2 * half, 2 * half + 2)
+                nc.sync.dma_start(out=x_sb[:, js, :], in_=x_view[c][:, js, :])
+            x_tiles[c] = x_sb
+
+        w_codes = consts.tile([P, GATES, PASSES, D_OUT], U32, align_bytes=64)
+        w_planes = consts.tile([P, GATES, PASSES * D_OUT], U8, align_bytes=64)
+        nc.vector.memset(w_planes[:].bitcast(I32), 0)
+
+        def load_weight(gate):
+            nc.sync.dma_start(
+                out=w_codes[:, gate, :, :].bitcast(I32),
+                in_=gate_words[gate].rearrange("g p n t -> p g (n t)").bitcast(I32),
+            )
+            scale_words = gate_scales[gate].bitcast(I32)
+            for r in range(4):
+                nc.sync.dma_start(
+                    out=w_planes[r:P:32, gate, :].bitcast(I32).rearrange("q (g n) -> q g n", g=PASSES),
+                    in_=scale_words[:, r:16:4, :].rearrange("g q n -> q g n"),
+                )
+
+        load_chunk(0)
+        load_chunk(1)
+        for gate in range(GATES):
+            load_weight(gate)
+        for c in range(2, N_CHUNKS):
+            load_chunk(c)
+
+        def transpose_pass(c, g):
+            grouped = grouped_pool.tile([P, PACK * CHUNK], BF16, align_bytes=64)
+            grouped_words = grouped[:].bitcast(F32).rearrange("p (n u) -> p n u", u=2)
+            for half in range(2):
+                xt = banks.tile([P, 2, 2 * P], F32, tag="bank")
+                for jj in range(2):
+                    row_words = x_tiles[c][:, 2 * half + jj, :].bitcast(F32)
+                    for u in range(2):
+                        nc.tensor.transpose(
+                            out=xt[:, u, jj * P : (jj + 1) * P],
+                            in_=row_words[:, WORDS * g + u : WORDS * (g + 1) : 2],
+                            identity=ident[:],
+                        )
+                nc.vector.tensor_copy(
+                    out=grouped_words[:, 2 * P * half : 2 * P * (half + 1), :],
+                    in_=xt[:].rearrange("p u n -> p n u"),
+                )
+            grouped_tiles[(c, g)] = grouped
+
+        def quantise_pass(c, g):
+            x_codes = operand_pool.tile([P, CHUNK], U32, align_bytes=64)
+            x_plane = operand_pool.tile([P, CHUNK], U8, align_bytes=64)
+            nc.vector.quantize_mx(out=x_codes[:].bitcast(FP8X4), scales=x_plane[:], in_=grouped_tiles[(c, g)][:])
+            code_tiles[(c, g)] = x_codes
+            plane_tiles[(c, g)] = x_plane
+
+        def gates(c):
+            for gate in range(GATES):
+                gate_sb = gate_pool.tile([P, HALVES, CHUNK], F32, tag="gate%d" % gate)
+                for h in range(HALVES):
+                    feats = slice(h * P, (h + 1) * P)
+                    acc = banks.tile([P, CHUNK], F32, tag="bank")
+                    for g in range(PASSES):
+                        nc.tensor.matmul_mx(
+                            out=acc[:],
+                            lhsT=w_codes[:, gate, g, feats].bitcast(FP8X4),
+                            lhsT_scale=w_planes[:, gate, g * D_OUT + h * P : g * D_OUT + (h + 1) * P],
+                            rhs=code_tiles[(c, g)][:].bitcast(FP8X4),
+                            rhs_scale=plane_tiles[(c, g)][:],
+                            start=(g == 0),
+                            stop=(g == PASSES - 1),
+                        )
+                    column = HALVES * gate + h
+                    nc.scalar.activation(
+                        out=gate_sb[:, h, :],
+                        in_=acc[:],
+                        func=gate_funcs[gate],
+                        bias=bias_cols[:, column : column + 1],
+                        scale=1.0,
+                    )
+                gate_tiles[(c, gate)] = gate_sb
+
+        def state_product(c):
+            state = gate_pool.tile([P, HALVES, CHUNK], F32)
+            nc.vector.tensor_mul(out=state[:], in0=gate_tiles[(c, 1)][:], in1=gate_tiles[(c, 0)][:])
+            state_tiles[c] = state
+
+        def tanh_state(c):
+            tanh_sb = gate_pool.tile([P, HALVES, CHUNK], F32)
+            nc.scalar.activation(out=tanh_sb[:], in_=state_tiles[c][:], func=FUNC.Tanh)
+            tanh_tiles[c] = tanh_sb
+
+        def output_product(c):
+            result = gate_pool.tile([P, HALVES, CHUNK], F32)
+            nc.vector.tensor_mul(out=result[:], in0=tanh_tiles[c][:], in1=gate_tiles[(c, 2)][:])
+            result_tiles[c] = result
+
+        def transpose_out(c):
+            out_sb = out_pool.tile([P, ROWS, D_OUT], F32)
+            for half in range(2):
+                ot = banks.tile([P, 2, D_OUT], F32, tag="bank")
+                for jj in range(2):
+                    j = 2 * half + jj
+                    for h in range(HALVES):
+                        nc.tensor.transpose(
+                            out=ot[:, jj, h * P : (h + 1) * P],
+                            in_=result_tiles[c][:, h, j * P : (j + 1) * P],
+                            identity=ident[:],
+                        )
+                nc.scalar.copy(out=out_sb[:, 2 * half : 2 * half + 2, :], in_=ot[:])
+            nc.sync.dma_start(out=out_view[c], in_=out_sb[:])
+
+        for g in range(PASSES):
+            transpose_pass(0, g)
+
+        bias_bank = banks.tile([P, CHUNK], F32, tag="bank")
+        nc.tensor.transpose(out=bias_bank[:, 0:P], in_=bias_rows_f32[:], identity=ident[:])
+        bias_cols = consts.tile([P, GATES * HALVES], F32)
+        nc.vector.tensor_copy(out=bias_cols[:], in_=bias_bank[:, 0 : GATES * HALVES])
+
+        for g in range(PASSES):
+            quantise_pass(0, g)
+
+        for c in range(N_CHUNKS + 2):
+            if 1 <= c <= N_CHUNKS:
+                tanh_state(c - 1)
+            if c + 1 < N_CHUNKS:
+                for g in range(PASSES):
+                    transpose_pass(c + 1, g)
+                quantise_pass(c + 1, 0)
+            if c >= 2:
+                transpose_out(c - 2)
+            if 1 <= c <= N_CHUNKS:
+                output_product(c - 1)
+            if c + 1 < N_CHUNKS:
+                quantise_pass(c + 1, 1)
+            if c < N_CHUNKS:
+                gates(c)
+                state_product(c)

@@ -21,7 +21,9 @@ HALVES = D_OUT // P
 CHUNK = 512
 ROWS = CHUNK // P
 N_CHUNKS = BATCH // CHUNK
-WORDS = K_PASS // 2
+N_OPERANDS = N_CHUNKS * PASSES
+N_STEPS = N_CHUNKS * HALVES
+LOOKAHEAD = 3
 
 FLOPS = 2 * BATCH * D_IN * GATES * D_OUT
 
@@ -40,11 +42,11 @@ def tile_lstm_pa_t_kernel(
 
     with ExitStack() as stack:
         consts = stack.enter_context(tc.tile_pool(name="consts", bufs=1))
-        x_pool = stack.enter_context(tc.tile_pool(name="x", bufs=N_CHUNKS))
+        x_pool = stack.enter_context(tc.tile_pool(name="x", bufs=N_OPERANDS))
         grouped_pool = stack.enter_context(tc.tile_pool(name="grouped", bufs=4))
-        operand_pool = stack.enter_context(tc.tile_pool(name="operand", bufs=4))
-        gate_pool = stack.enter_context(tc.tile_pool(name="gate", bufs=3))
-        out_pool = stack.enter_context(tc.tile_pool(name="out", bufs=3))
+        operand_pool = stack.enter_context(tc.tile_pool(name="operand", bufs=PASSES + LOOKAHEAD + 1))
+        gate_pool = stack.enter_context(tc.tile_pool(name="gate", bufs=4))
+        out_pool = stack.enter_context(tc.tile_pool(name="out", bufs=6))
         banks = stack.enter_context(tc.psum_pool(name="banks", bufs=8))
         stack.enter_context(tc.manual_schedule())
 
@@ -62,29 +64,27 @@ def tile_lstm_pa_t_kernel(
                 in_=gate_biases[gate].rearrange("(h f) -> h f", h=HALVES),
             )
 
-        bias_rows_f32 = consts.tile([P, P], F32)
-        nc.gpsimd.tensor_copy(out=bias_rows_f32[:], in_=bias_rows[:])
-
         warm = consts.tile([P, 2], F32)
         nc.vector.memset(warm[:], 0.0)
         nc.scalar.activation(out=warm[:, 1:2], in_=warm[:, 0:1], func=FUNC.Sigmoid)
 
-        def load_chunk(c):
-            x_sb = x_pool.tile([P, ROWS, D_IN], BF16)
-            for half in range(2):
-                js = slice(2 * half, 2 * half + 2)
-                nc.sync.dma_start(out=x_sb[:, js, :], in_=x_view[c][:, js, :])
-            x_tiles[c] = x_sb
+        def load_operand(u):
+            c, g = divmod(u, PASSES)
+            x_sb = x_pool.tile([P, ROWS, K_PASS], BF16)
+            nc.sync.dma_start(out=x_sb[:], in_=x_view[c][:, :, g * K_PASS : (g + 1) * K_PASS])
+            x_tiles[u] = x_sb
 
         w_codes = consts.tile([P, GATES, PASSES, D_OUT], U32, align_bytes=64)
+        for gate in range(GATES):
+            nc.gpsimd.dma_start(
+                out=w_codes[:, gate, :, :].bitcast(F32),
+                in_=gate_words[gate].rearrange("g p n t -> p g (n t)").bitcast(F32),
+            )
+
         w_planes = consts.tile([P, GATES, PASSES * D_OUT], U8, align_bytes=64)
         nc.vector.memset(w_planes[:].bitcast(I32), 0)
 
-        def load_weight(gate):
-            nc.sync.dma_start(
-                out=w_codes[:, gate, :, :].bitcast(I32),
-                in_=gate_words[gate].rearrange("g p n t -> p g (n t)").bitcast(I32),
-            )
+        def load_scales(gate):
             scale_words = gate_scales[gate].bitcast(I32)
             for r in range(4):
                 nc.sync.dma_start(
@@ -92,119 +92,112 @@ def tile_lstm_pa_t_kernel(
                     in_=scale_words[:, r:16:4, :].rearrange("g q n -> q g n"),
                 )
 
-        load_chunk(0)
-        load_chunk(1)
+        for u in range(LOOKAHEAD):
+            load_operand(u)
         for gate in range(GATES):
-            load_weight(gate)
-        for c in range(2, N_CHUNKS):
-            load_chunk(c)
+            load_scales(gate)
+        for u in range(LOOKAHEAD, N_OPERANDS):
+            load_operand(u)
 
-        def transpose_pass(c, g):
+        bias_rows_f32 = consts.tile([P, P], F32)
+        nc.vector.tensor_copy(out=bias_rows_f32[:], in_=bias_rows[:])
+
+        def transpose_operand(u):
             grouped = grouped_pool.tile([P, PACK * CHUNK], BF16, align_bytes=64)
-            grouped_words = grouped[:].bitcast(F32).rearrange("p (n u) -> p n u", u=2)
+            grouped_words = grouped[:].bitcast(F32).rearrange("p (n w) -> p n w", w=2)
             for half in range(2):
                 xt = banks.tile([P, 2, 2 * P], F32, tag="bank")
                 for jj in range(2):
-                    row_words = x_tiles[c][:, 2 * half + jj, :].bitcast(F32)
-                    for u in range(2):
+                    row_words = x_tiles[u][:, 2 * half + jj, :].bitcast(F32)
+                    for w in range(2):
                         nc.tensor.transpose(
-                            out=xt[:, u, jj * P : (jj + 1) * P],
-                            in_=row_words[:, WORDS * g + u : WORDS * (g + 1) : 2],
+                            out=xt[:, w, jj * P : (jj + 1) * P],
+                            in_=row_words[:, w : K_PASS // 2 : 2],
                             identity=ident[:],
                         )
-                nc.vector.tensor_copy(
+                copy = nc.vector.tensor_copy if half == 0 else nc.scalar.copy
+                copy(
                     out=grouped_words[:, 2 * P * half : 2 * P * (half + 1), :],
-                    in_=xt[:].rearrange("p u n -> p n u"),
+                    in_=xt[:].rearrange("p w n -> p n w"),
                 )
-            grouped_tiles[(c, g)] = grouped
+            grouped_tiles[u] = grouped
 
-        def quantise_pass(c, g):
+        def quantise_operand(u):
             x_codes = operand_pool.tile([P, CHUNK], U32, align_bytes=64)
             x_plane = operand_pool.tile([P, CHUNK], U8, align_bytes=64)
-            nc.vector.quantize_mx(out=x_codes[:].bitcast(FP8X4), scales=x_plane[:], in_=grouped_tiles[(c, g)][:])
-            code_tiles[(c, g)] = x_codes
-            plane_tiles[(c, g)] = x_plane
+            nc.vector.quantize_mx(out=x_codes[:].bitcast(FP8X4), scales=x_plane[:], in_=grouped_tiles[u][:])
+            code_tiles[u] = x_codes
+            plane_tiles[u] = x_plane
 
-        def gates(c):
+        def gates(t):
+            c, h = divmod(t, HALVES)
             for gate in range(GATES):
-                gate_sb = gate_pool.tile([P, HALVES, CHUNK], F32, tag="gate%d" % gate)
-                for h in range(HALVES):
-                    feats = slice(h * P, (h + 1) * P)
-                    acc = banks.tile([P, CHUNK], F32, tag="bank")
-                    for g in range(PASSES):
-                        nc.tensor.matmul_mx(
-                            out=acc[:],
-                            lhsT=w_codes[:, gate, g, feats].bitcast(FP8X4),
-                            lhsT_scale=w_planes[:, gate, g * D_OUT + h * P : g * D_OUT + (h + 1) * P],
-                            rhs=code_tiles[(c, g)][:].bitcast(FP8X4),
-                            rhs_scale=plane_tiles[(c, g)][:],
-                            start=(g == 0),
-                            stop=(g == PASSES - 1),
-                        )
-                    column = HALVES * gate + h
-                    nc.scalar.activation(
-                        out=gate_sb[:, h, :],
-                        in_=acc[:],
-                        func=gate_funcs[gate],
-                        bias=bias_cols[:, column : column + 1],
-                        scale=1.0,
+                acc = banks.tile([P, CHUNK], F32, tag="bank")
+                for g in range(PASSES):
+                    nc.tensor.matmul_mx(
+                        out=acc[:],
+                        lhsT=w_codes[:, gate, g, h * P : (h + 1) * P].bitcast(FP8X4),
+                        lhsT_scale=w_planes[:, gate, g * D_OUT + h * P : g * D_OUT + (h + 1) * P],
+                        rhs=code_tiles[PASSES * c + g][:].bitcast(FP8X4),
+                        rhs_scale=plane_tiles[PASSES * c + g][:],
+                        start=(g == 0),
+                        stop=(g == PASSES - 1),
                     )
-                gate_tiles[(c, gate)] = gate_sb
+                gate_sb = gate_pool.tile([P, CHUNK], F32, tag="gate%d" % gate)
+                column = HALVES * gate + h
+                nc.scalar.activation(
+                    out=gate_sb[:],
+                    in_=acc[:],
+                    func=gate_funcs[gate],
+                    bias=bias_cols[:, column : column + 1],
+                    scale=1.0,
+                )
+                gate_tiles[(t, gate)] = gate_sb
 
-        def state_product(c):
-            state = gate_pool.tile([P, HALVES, CHUNK], F32)
-            nc.vector.tensor_mul(out=state[:], in0=gate_tiles[(c, 1)][:], in1=gate_tiles[(c, 0)][:])
-            state_tiles[c] = state
+        def state_product(t):
+            state = gate_pool.tile([P, CHUNK], F32)
+            nc.vector.tensor_mul(out=state[:], in0=gate_tiles[(t, 1)][:], in1=gate_tiles[(t, 0)][:])
+            state_tiles[t] = state
 
-        def tanh_state(c):
-            tanh_sb = gate_pool.tile([P, HALVES, CHUNK], F32)
-            nc.scalar.activation(out=tanh_sb[:], in_=state_tiles[c][:], func=FUNC.Tanh)
-            tanh_tiles[c] = tanh_sb
+        def tanh_state(t):
+            tanh_sb = gate_pool.tile([P, CHUNK], F32)
+            nc.scalar.activation(out=tanh_sb[:], in_=state_tiles[t][:], func=FUNC.Tanh)
+            tanh_tiles[t] = tanh_sb
 
-        def output_product(c):
-            result = gate_pool.tile([P, HALVES, CHUNK], F32)
-            nc.vector.tensor_mul(out=result[:], in0=tanh_tiles[c][:], in1=gate_tiles[(c, 2)][:])
-            result_tiles[c] = result
+        def output_product(t):
+            result = gate_pool.tile([P, CHUNK], F32)
+            nc.vector.tensor_mul(out=result[:], in0=tanh_tiles[t][:], in1=gate_tiles[(t, 2)][:])
+            result_tiles[t] = result
 
-        def transpose_out(c):
-            out_sb = out_pool.tile([P, ROWS, D_OUT], F32)
-            for half in range(2):
-                ot = banks.tile([P, 2, D_OUT], F32, tag="bank")
-                for jj in range(2):
-                    j = 2 * half + jj
-                    for h in range(HALVES):
-                        nc.tensor.transpose(
-                            out=ot[:, jj, h * P : (h + 1) * P],
-                            in_=result_tiles[c][:, h, j * P : (j + 1) * P],
-                            identity=ident[:],
-                        )
-                nc.scalar.copy(out=out_sb[:, 2 * half : 2 * half + 2, :], in_=ot[:])
-            nc.sync.dma_start(out=out_view[c], in_=out_sb[:])
+        def transpose_out(t):
+            c, h = divmod(t, HALVES)
+            ot = banks.tile([P, ROWS, P], F32, tag="bank")
+            for j in range(ROWS):
+                nc.tensor.transpose(out=ot[:, j, :], in_=result_tiles[t][:, j * P : (j + 1) * P], identity=ident[:])
+            out_sb = out_pool.tile([P, ROWS, P], F32)
+            nc.vector.tensor_copy(out=out_sb[:], in_=ot[:])
+            nc.sync.dma_start(out=out_view[c][:, :, h * P : (h + 1) * P], in_=out_sb[:])
 
-        for g in range(PASSES):
-            transpose_pass(0, g)
-
+        for u in range(LOOKAHEAD):
+            transpose_operand(u)
+            if u >= 1:
+                quantise_operand(u - 1)
         bias_bank = banks.tile([P, CHUNK], F32, tag="bank")
         nc.tensor.transpose(out=bias_bank[:, 0:P], in_=bias_rows_f32[:], identity=ident[:])
         bias_cols = consts.tile([P, GATES * HALVES], F32)
         nc.vector.tensor_copy(out=bias_cols[:], in_=bias_bank[:, 0 : GATES * HALVES])
+        quantise_operand(LOOKAHEAD - 1)
 
-        for g in range(PASSES):
-            quantise_pass(0, g)
-
-        for c in range(N_CHUNKS + 2):
-            if 1 <= c <= N_CHUNKS:
-                tanh_state(c - 1)
-            if c + 1 < N_CHUNKS:
-                for g in range(PASSES):
-                    transpose_pass(c + 1, g)
-                quantise_pass(c + 1, 0)
-            if c >= 2:
-                transpose_out(c - 2)
-            if 1 <= c <= N_CHUNKS:
-                output_product(c - 1)
-            if c + 1 < N_CHUNKS:
-                quantise_pass(c + 1, 1)
-            if c < N_CHUNKS:
-                gates(c)
-                state_product(c)
+        for t in range(N_STEPS + 1):
+            if t < N_STEPS:
+                gates(t)
+                state_product(t)
+                tanh_state(t)
+            if t + LOOKAHEAD < N_OPERANDS:
+                transpose_operand(t + LOOKAHEAD)
+            if t < N_STEPS:
+                output_product(t)
+            if t >= 1:
+                transpose_out(t - 1)
+            if t + LOOKAHEAD < N_OPERANDS:
+                quantise_operand(t + LOOKAHEAD)

@@ -21,9 +21,7 @@ HALVES = D_OUT // P
 CHUNK = 512
 ROWS = CHUNK // P
 N_CHUNKS = BATCH // CHUNK
-N_OPERANDS = N_CHUNKS * PASSES
-N_STEPS = N_CHUNKS * HALVES
-LOOKAHEAD = 3
+WORDS = K_PASS // 2
 
 FLOPS = 2 * BATCH * D_IN * GATES * D_OUT
 
@@ -42,11 +40,11 @@ def tile_lstm_pa_t_kernel(
 
     with ExitStack() as stack:
         consts = stack.enter_context(tc.tile_pool(name="consts", bufs=1))
-        x_pool = stack.enter_context(tc.tile_pool(name="x", bufs=N_OPERANDS))
+        x_pool = stack.enter_context(tc.tile_pool(name="x", bufs=N_CHUNKS))
         grouped_pool = stack.enter_context(tc.tile_pool(name="grouped", bufs=4))
-        operand_pool = stack.enter_context(tc.tile_pool(name="operand", bufs=PASSES + LOOKAHEAD + 1))
-        gate_pool = stack.enter_context(tc.tile_pool(name="gate", bufs=4))
-        out_pool = stack.enter_context(tc.tile_pool(name="out", bufs=6))
+        operand_pool = stack.enter_context(tc.tile_pool(name="operand", bufs=4))
+        gate_pool = stack.enter_context(tc.tile_pool(name="gate", bufs=3))
+        out_pool = stack.enter_context(tc.tile_pool(name="out", bufs=3))
         banks = stack.enter_context(tc.psum_pool(name="banks", bufs=8))
         stack.enter_context(tc.manual_schedule())
 
@@ -64,27 +62,29 @@ def tile_lstm_pa_t_kernel(
                 in_=gate_biases[gate].rearrange("(h f) -> h f", h=HALVES),
             )
 
+        bias_rows_f32 = consts.tile([P, P], F32)
+        nc.gpsimd.tensor_copy(out=bias_rows_f32[:], in_=bias_rows[:])
+
         warm = consts.tile([P, 2], F32)
         nc.vector.memset(warm[:], 0.0)
         nc.scalar.activation(out=warm[:, 1:2], in_=warm[:, 0:1], func=FUNC.Sigmoid)
 
-        def load_operand(u):
-            c, g = divmod(u, PASSES)
-            x_sb = x_pool.tile([P, ROWS, K_PASS], BF16)
-            nc.sync.dma_start(out=x_sb[:], in_=x_view[c][:, :, g * K_PASS : (g + 1) * K_PASS])
-            x_tiles[u] = x_sb
+        def load_chunk(c):
+            x_sb = x_pool.tile([P, ROWS, D_IN], BF16)
+            for half in range(2):
+                js = slice(2 * half, 2 * half + 2)
+                nc.sync.dma_start(out=x_sb[:, js, :], in_=x_view[c][:, js, :])
+            x_tiles[c] = x_sb
 
         w_codes = consts.tile([P, GATES, PASSES, D_OUT], U32, align_bytes=64)
-        for gate in range(GATES):
-            nc.gpsimd.dma_start(
-                out=w_codes[:, gate, :, :].bitcast(F32),
-                in_=gate_words[gate].rearrange("g p n t -> p g (n t)").bitcast(F32),
-            )
-
         w_planes = consts.tile([P, GATES, PASSES * D_OUT], U8, align_bytes=64)
         nc.vector.memset(w_planes[:].bitcast(I32), 0)
 
-        def load_scales(gate):
+        def load_weight(gate):
+            nc.sync.dma_start(
+                out=w_codes[:, gate, :, :].bitcast(I32),
+                in_=gate_words[gate].rearrange("g p n t -> p g (n t)").bitcast(I32),
+            )
             scale_words = gate_scales[gate].bitcast(I32)
             for r in range(4):
                 nc.sync.dma_start(
@@ -92,112 +92,125 @@ def tile_lstm_pa_t_kernel(
                     in_=scale_words[:, r:16:4, :].rearrange("g q n -> q g n"),
                 )
 
-        for u in range(LOOKAHEAD):
-            load_operand(u)
+        load_chunk(0)
+        load_chunk(1)
         for gate in range(GATES):
-            load_scales(gate)
-        for u in range(LOOKAHEAD, N_OPERANDS):
-            load_operand(u)
+            load_weight(gate)
+        for c in range(2, N_CHUNKS):
+            load_chunk(c)
 
-        bias_rows_f32 = consts.tile([P, P], F32)
-        nc.vector.tensor_copy(out=bias_rows_f32[:], in_=bias_rows[:])
-
-        def transpose_operand(u):
+        def transpose_pass(c, g):
             grouped = grouped_pool.tile([P, PACK * CHUNK], BF16, align_bytes=64)
-            grouped_words = grouped[:].bitcast(F32).rearrange("p (n w) -> p n w", w=2)
+            grouped_words = grouped[:].bitcast(F32).rearrange("p (n u) -> p n u", u=2)
+            copy_out = nc.vector.tensor_copy if g == 0 else nc.scalar.copy
             for half in range(2):
                 xt = banks.tile([P, 2, 2 * P], F32, tag="bank")
                 for jj in range(2):
-                    row_words = x_tiles[u][:, 2 * half + jj, :].bitcast(F32)
-                    for w in range(2):
+                    row_words = x_tiles[c][:, 2 * half + jj, :].bitcast(F32)
+                    for u in range(2):
                         nc.tensor.transpose(
-                            out=xt[:, w, jj * P : (jj + 1) * P],
-                            in_=row_words[:, w : K_PASS // 2 : 2],
+                            out=xt[:, u, jj * P : (jj + 1) * P],
+                            in_=row_words[:, WORDS * g + u : WORDS * (g + 1) : 2],
                             identity=ident[:],
                         )
-                copy = nc.vector.tensor_copy if half == 0 else nc.scalar.copy
-                copy(
+                copy_out(
                     out=grouped_words[:, 2 * P * half : 2 * P * (half + 1), :],
-                    in_=xt[:].rearrange("p w n -> p n w"),
+                    in_=xt[:].rearrange("p u n -> p n u"),
                 )
-            grouped_tiles[u] = grouped
+            grouped_tiles[(c, g)] = grouped
 
-        def quantise_operand(u):
+        def quantise_pass(c, g):
             x_codes = operand_pool.tile([P, CHUNK], U32, align_bytes=64)
             x_plane = operand_pool.tile([P, CHUNK], U8, align_bytes=64)
-            nc.vector.quantize_mx(out=x_codes[:].bitcast(FP8X4), scales=x_plane[:], in_=grouped_tiles[u][:])
-            code_tiles[u] = x_codes
-            plane_tiles[u] = x_plane
+            nc.vector.quantize_mx(out=x_codes[:].bitcast(FP8X4), scales=x_plane[:], in_=grouped_tiles[(c, g)][:])
+            code_tiles[(c, g)] = x_codes
+            plane_tiles[(c, g)] = x_plane
 
-        def gates(t):
-            c, h = divmod(t, HALVES)
+        def gates(c):
             for gate in range(GATES):
-                acc = banks.tile([P, CHUNK], F32, tag="bank")
-                for g in range(PASSES):
-                    nc.tensor.matmul_mx(
-                        out=acc[:],
-                        lhsT=w_codes[:, gate, g, h * P : (h + 1) * P].bitcast(FP8X4),
-                        lhsT_scale=w_planes[:, gate, g * D_OUT + h * P : g * D_OUT + (h + 1) * P],
-                        rhs=code_tiles[PASSES * c + g][:].bitcast(FP8X4),
-                        rhs_scale=plane_tiles[PASSES * c + g][:],
-                        start=(g == 0),
-                        stop=(g == PASSES - 1),
+                gate_sb = gate_pool.tile([P, HALVES, CHUNK], F32, tag="gate%d" % gate)
+                for h in range(HALVES):
+                    feats = slice(h * P, (h + 1) * P)
+                    acc = banks.tile([P, CHUNK], F32, tag="bank")
+                    for g in range(PASSES):
+                        nc.tensor.matmul_mx(
+                            out=acc[:],
+                            lhsT=w_codes[:, gate, g, feats].bitcast(FP8X4),
+                            lhsT_scale=w_planes[:, gate, g * D_OUT + h * P : g * D_OUT + (h + 1) * P],
+                            rhs=code_tiles[(c, g)][:].bitcast(FP8X4),
+                            rhs_scale=plane_tiles[(c, g)][:],
+                            start=(g == 0),
+                            stop=(g == PASSES - 1),
+                        )
+                    column = HALVES * gate + h
+                    nc.scalar.activation(
+                        out=gate_sb[:, h, :],
+                        in_=acc[:],
+                        func=gate_funcs[gate],
+                        bias=bias_cols[:, column : column + 1],
+                        scale=1.0,
                     )
-                gate_sb = gate_pool.tile([P, CHUNK], F32, tag="gate%d" % gate)
-                column = HALVES * gate + h
-                nc.scalar.activation(
-                    out=gate_sb[:],
-                    in_=acc[:],
-                    func=gate_funcs[gate],
-                    bias=bias_cols[:, column : column + 1],
-                    scale=1.0,
-                )
-                gate_tiles[(t, gate)] = gate_sb
+                gate_tiles[(c, gate)] = gate_sb
 
-        def state_product(t):
-            state = gate_pool.tile([P, CHUNK], F32)
-            nc.vector.tensor_mul(out=state[:], in0=gate_tiles[(t, 1)][:], in1=gate_tiles[(t, 0)][:])
-            state_tiles[t] = state
+        def state_product(c, h):
+            if h == 0:
+                state = gate_pool.tile([P, HALVES, CHUNK], F32)
+                state_tiles[c] = state
+            nc.vector.tensor_mul(
+                out=state_tiles[c][:, h, :], in0=gate_tiles[(c, 1)][:, h, :], in1=gate_tiles[(c, 0)][:, h, :]
+            )
 
-        def tanh_state(t):
-            tanh_sb = gate_pool.tile([P, CHUNK], F32)
-            nc.scalar.activation(out=tanh_sb[:], in_=state_tiles[t][:], func=FUNC.Tanh)
-            tanh_tiles[t] = tanh_sb
+        def tanh_state(c, h):
+            if h == 0:
+                tanh_sb = gate_pool.tile([P, HALVES, CHUNK], F32)
+                tanh_tiles[c] = tanh_sb
+            nc.scalar.activation(out=tanh_tiles[c][:, h, :], in_=state_tiles[c][:, h, :], func=FUNC.Tanh)
 
-        def output_product(t):
-            result = gate_pool.tile([P, CHUNK], F32)
-            nc.vector.tensor_mul(out=result[:], in0=tanh_tiles[t][:], in1=gate_tiles[(t, 2)][:])
-            result_tiles[t] = result
+        def output_product(c, h):
+            if h == 0:
+                result = gate_pool.tile([P, HALVES, CHUNK], F32)
+                result_tiles[c] = result
+            nc.vector.tensor_mul(
+                out=result_tiles[c][:, h, :], in0=tanh_tiles[c][:, h, :], in1=gate_tiles[(c, 2)][:, h, :]
+            )
 
-        def transpose_out(t):
-            c, h = divmod(t, HALVES)
-            ot = banks.tile([P, ROWS, P], F32, tag="bank")
-            for j in range(ROWS):
-                nc.tensor.transpose(out=ot[:, j, :], in_=result_tiles[t][:, j * P : (j + 1) * P], identity=ident[:])
-            out_sb = out_pool.tile([P, ROWS, P], F32)
-            nc.vector.tensor_copy(out=out_sb[:], in_=ot[:])
-            nc.sync.dma_start(out=out_view[c][:, :, h * P : (h + 1) * P], in_=out_sb[:])
+        def transpose_out(c):
+            out_sb = out_pool.tile([P, ROWS, D_OUT], F32)
+            for h in range(HALVES):
+                ot = banks.tile([P, ROWS, P], F32, tag="bank")
+                for j in range(ROWS):
+                    nc.tensor.transpose(
+                        out=ot[:, j, :], in_=result_tiles[c][:, h, j * P : (j + 1) * P], identity=ident[:]
+                    )
+                nc.vector.tensor_copy(out=out_sb[:, :, h * P : (h + 1) * P], in_=ot[:])
+            nc.sync.dma_start(out=out_view[c], in_=out_sb[:])
 
-        for u in range(LOOKAHEAD):
-            transpose_operand(u)
-            if u >= 1:
-                quantise_operand(u - 1)
+        for g in range(PASSES):
+            transpose_pass(0, g)
+
         bias_bank = banks.tile([P, CHUNK], F32, tag="bank")
         nc.tensor.transpose(out=bias_bank[:, 0:P], in_=bias_rows_f32[:], identity=ident[:])
         bias_cols = consts.tile([P, GATES * HALVES], F32)
         nc.vector.tensor_copy(out=bias_cols[:], in_=bias_bank[:, 0 : GATES * HALVES])
-        quantise_operand(LOOKAHEAD - 1)
 
-        for t in range(N_STEPS + 1):
-            if t < N_STEPS:
-                gates(t)
-                state_product(t)
-                tanh_state(t)
-            if t + LOOKAHEAD < N_OPERANDS:
-                transpose_operand(t + LOOKAHEAD)
-            if t < N_STEPS:
-                output_product(t)
-            if t >= 1:
-                transpose_out(t - 1)
-            if t + LOOKAHEAD < N_OPERANDS:
-                quantise_operand(t + LOOKAHEAD)
+        for g in range(PASSES):
+            quantise_pass(0, g)
+
+        for c in range(N_CHUNKS + 2):
+            if 1 <= c <= N_CHUNKS:
+                for h in range(HALVES):
+                    tanh_state(c - 1, h)
+            if c >= 2:
+                transpose_out(c - 2)
+            if c + 1 < N_CHUNKS:
+                for g in range(PASSES):
+                    transpose_pass(c + 1, g)
+            for half in range(2):
+                if 1 <= c <= N_CHUNKS:
+                    output_product(c - 1, half)
+                if c + 1 < N_CHUNKS:
+                    quantise_pass(c + 1, half)
+            if c < N_CHUNKS:
+                gates(c)
+                for h in range(HALVES):
+                    state_product(c, h)

@@ -22,6 +22,10 @@ CHUNK = 512
 ROWS = CHUNK // P
 N_CHUNKS = BATCH // CHUNK
 WORDS = K_PASS // 2
+BLOCK = 32
+QUADS = P // BLOCK
+ROW_BLOCKS = CHUNK // BLOCK
+RUN = HALVES * BLOCK
 
 FLOPS = 2 * BATCH * D_IN * GATES * D_OUT
 
@@ -35,8 +39,8 @@ def tile_lstm_pa_t_kernel(
     gate_biases = [bxi, bxc, bxo]
     gate_funcs = [FUNC.Sigmoid, FUNC.Tanh, FUNC.Sigmoid]
 
-    x_view = x.rearrange("(c p j) k -> c p j k", p=P, j=ROWS)
-    out_view = out.rearrange("(c p j) f -> c p j f", p=P, j=ROWS)
+    x_view = x.rearrange("(c j p) k -> c p j k", p=P, j=ROWS)
+    out_view = out.rearrange("(c R r) (F e) -> c F r R e", R=ROW_BLOCKS, r=BLOCK, F=QUADS)
 
     with ExitStack() as stack:
         consts = stack.enter_context(tc.tile_pool(name="consts", bufs=1))
@@ -58,8 +62,8 @@ def tile_lstm_pa_t_kernel(
         nc.vector.memset(bias_rows[:], 0.0)
         for gate in range(GATES):
             nc.scalar.dma_start(
-                out=bias_rows[HALVES * gate : HALVES * (gate + 1), :],
-                in_=gate_biases[gate].rearrange("(h f) -> h f", h=HALVES),
+                out=bias_rows[HALVES * gate : HALVES * (gate + 1), :].rearrange("h (F f) -> h F f", F=QUADS),
+                in_=gate_biases[gate].rearrange("(F h f) -> h F f", F=QUADS, h=HALVES),
             )
 
         bias_rows_f32 = consts.tile([P, P], F32)
@@ -76,20 +80,39 @@ def tile_lstm_pa_t_kernel(
                 nc.sync.dma_start(out=x_sb[:, js, :], in_=x_view[c][:, js, :])
             x_tiles[c] = x_sb
 
+        w_codes_in = consts.tile([P, GATES, PASSES, D_OUT], U32, align_bytes=64)
         w_codes = consts.tile([P, GATES, PASSES, D_OUT], U32, align_bytes=64)
+        w_planes_in = consts.tile([P, GATES, PASSES * D_OUT], U8, align_bytes=64)
         w_planes = consts.tile([P, GATES, PASSES * D_OUT], U8, align_bytes=64)
-        nc.vector.memset(w_planes[:].bitcast(I32), 0)
+        nc.vector.memset(w_planes_in[:].bitcast(I32), 0)
 
         def load_weight(gate):
             nc.sync.dma_start(
-                out=w_codes[:, gate, :, :].bitcast(I32),
+                out=w_codes_in[:, gate, :, :].bitcast(I32),
                 in_=gate_words[gate].rearrange("g p n t -> p g (n t)").bitcast(I32),
             )
             scale_words = gate_scales[gate].bitcast(I32)
             for r in range(4):
                 nc.sync.dma_start(
-                    out=w_planes[r:P:32, gate, :].bitcast(I32).rearrange("q (g n) -> q g n", g=PASSES),
+                    out=w_planes_in[r:P:32, gate, :].bitcast(I32).rearrange("q (g n) -> q g n", g=PASSES),
                     in_=scale_words[:, r:16:4, :].rearrange("g q n -> q g n"),
+                )
+
+        def permute_weight(gate):
+            for h in range(HALVES):
+                nc.vector.tensor_copy(
+                    out=w_codes[:, gate, :, h * P : (h + 1) * P].bitcast(I32).rearrange("p g (F f) -> p g F f", F=QUADS),
+                    in_=w_codes_in[:, gate, :, :].bitcast(I32).rearrange(
+                        "p g (F h f) -> p h g F f", F=QUADS, h=HALVES
+                    )[:, h],
+                )
+                nc.vector.tensor_copy(
+                    out=w_planes[:, gate, :].bitcast(I32).rearrange(
+                        "p (g h F w) -> p h g F w", g=PASSES, h=HALVES, F=QUADS
+                    )[:, h],
+                    in_=w_planes_in[:, gate, :].bitcast(I32).rearrange(
+                        "p (g F h w) -> p h g F w", g=PASSES, h=HALVES, F=QUADS
+                    )[:, h],
                 )
 
         load_chunk(0)
@@ -126,31 +149,30 @@ def tile_lstm_pa_t_kernel(
             code_tiles[(c, g)] = x_codes
             plane_tiles[(c, g)] = x_plane
 
-        def gates(c):
-            for gate in range(GATES):
+        def gate_half(c, gate, h):
+            if h == 0:
                 gate_sb = gate_pool.tile([P, HALVES, CHUNK], F32, tag="gate%d" % gate)
-                for h in range(HALVES):
-                    feats = slice(h * P, (h + 1) * P)
-                    acc = banks.tile([P, CHUNK], F32, tag="bank")
-                    for g in range(PASSES):
-                        nc.tensor.matmul_mx(
-                            out=acc[:],
-                            lhsT=w_codes[:, gate, g, feats].bitcast(FP8X4),
-                            lhsT_scale=w_planes[:, gate, g * D_OUT + h * P : g * D_OUT + (h + 1) * P],
-                            rhs=code_tiles[(c, g)][:].bitcast(FP8X4),
-                            rhs_scale=plane_tiles[(c, g)][:],
-                            start=(g == 0),
-                            stop=(g == PASSES - 1),
-                        )
-                    column = HALVES * gate + h
-                    nc.scalar.activation(
-                        out=gate_sb[:, h, :],
-                        in_=acc[:],
-                        func=gate_funcs[gate],
-                        bias=bias_cols[:, column : column + 1],
-                        scale=1.0,
-                    )
                 gate_tiles[(c, gate)] = gate_sb
+            feats = slice(h * P, (h + 1) * P)
+            acc = banks.tile([P, CHUNK], F32, tag="bank")
+            for g in range(PASSES):
+                nc.tensor.matmul_mx(
+                    out=acc[:],
+                    lhsT=w_codes[:, gate, g, feats].bitcast(FP8X4),
+                    lhsT_scale=w_planes[:, gate, g * D_OUT + h * P : g * D_OUT + (h + 1) * P],
+                    rhs=code_tiles[(c, g)][:].bitcast(FP8X4),
+                    rhs_scale=plane_tiles[(c, g)][:],
+                    start=(g == 0),
+                    stop=(g == PASSES - 1),
+                )
+            column = HALVES * gate + h
+            nc.scalar.activation(
+                out=gate_tiles[(c, gate)][:, h, :],
+                in_=acc[:],
+                func=gate_funcs[gate],
+                bias=bias_cols[:, column : column + 1],
+                scale=1.0,
+            )
 
         def state_product(c, h):
             if h == 0:
@@ -168,22 +190,22 @@ def tile_lstm_pa_t_kernel(
 
         def output_product(c, h):
             if h == 0:
-                result = gate_pool.tile([P, HALVES, CHUNK], F32)
+                result = gate_pool.tile([P, ROW_BLOCKS, HALVES, BLOCK], F32, align_bytes=64)
                 result_tiles[c] = result
             nc.vector.tensor_mul(
-                out=result_tiles[c][:, h, :], in0=tanh_tiles[c][:, h, :], in1=gate_tiles[(c, 2)][:, h, :]
+                out=result_tiles[c][:, :, h, :],
+                in0=tanh_tiles[c][:, h, :].rearrange("p (R r) -> p R r", r=BLOCK),
+                in1=gate_tiles[(c, 2)][:, h, :].rearrange("p (R r) -> p R r", r=BLOCK),
             )
 
         def transpose_out(c):
-            out_sb = out_pool.tile([P, ROWS, D_OUT], F32)
-            for h in range(HALVES):
-                ot = banks.tile([P, ROWS, P], F32, tag="bank")
-                for j in range(ROWS):
-                    nc.tensor.transpose(
-                        out=ot[:, j, :], in_=result_tiles[c][:, h, j * P : (j + 1) * P], identity=ident[:]
-                    )
-                nc.vector.tensor_copy(out=out_sb[:, :, h * P : (h + 1) * P], in_=ot[:])
-            nc.sync.dma_start(out=out_view[c], in_=out_sb[:])
+            out_sb = out_pool.tile([P, ROW_BLOCKS * RUN], F32, align_bytes=64)
+            nc.vector.transpose(out=out_sb[:], in_=result_tiles[c][:].rearrange("p R h r -> p (R h r)"))
+            for quad in range(QUADS):
+                nc.sync.dma_start(
+                    out=out_view[c][quad],
+                    in_=out_sb[quad * BLOCK : (quad + 1) * BLOCK, :].rearrange("r (R e) -> r R e", e=RUN),
+                )
 
         for g in range(PASSES):
             transpose_pass(0, g)
@@ -200,17 +222,23 @@ def tile_lstm_pa_t_kernel(
             if 1 <= c <= N_CHUNKS:
                 for h in range(HALVES):
                     tanh_state(c - 1, h)
-            if c >= 2:
-                transpose_out(c - 2)
             if c + 1 < N_CHUNKS:
                 for g in range(PASSES):
                     transpose_pass(c + 1, g)
+            if c == 0:
+                for gate in range(GATES):
+                    permute_weight(gate)
+            if c >= 2:
+                transpose_out(c - 2)
             for half in range(2):
                 if 1 <= c <= N_CHUNKS:
                     output_product(c - 1, half)
                 if c + 1 < N_CHUNKS:
                     quantise_pass(c + 1, half)
             if c < N_CHUNKS:
-                gates(c)
                 for h in range(HALVES):
+                    gate_half(c, 0, h)
+                    gate_half(c, 1, h)
                     state_product(c, h)
+                for h in range(HALVES):
+                    gate_half(c, 2, h)

@@ -75,9 +75,12 @@ def tile_lstm_pa_t_kernel(
 
         def load_chunk(c):
             x_sb = x_pool.tile([P, ROWS, D_IN], BF16)
-            for half in range(2):
-                js = slice(2 * half, 2 * half + 2)
-                nc.sync.dma_start(out=x_sb[:, js, :], in_=x_view[c][:, js, :])
+            pieces = PASSES if c == 0 else 1
+            for piece in range(pieces):
+                ks = slice(piece * D_IN // pieces, (piece + 1) * D_IN // pieces)
+                for half in range(2):
+                    js = slice(2 * half, 2 * half + 2)
+                    nc.sync.dma_start(out=x_sb[:, js, ks], in_=x_view[c][:, js, ks])
             x_tiles[c] = x_sb
 
         w_codes_in = consts.tile([P, GATES, PASSES, D_OUT], U32, align_bytes=64)
@@ -125,7 +128,7 @@ def tile_lstm_pa_t_kernel(
         def transpose_pass(c, g):
             grouped = grouped_pool.tile([P, PACK * CHUNK], BF16, align_bytes=64)
             grouped_words = grouped[:].bitcast(F32).rearrange("p (n u) -> p n u", u=2)
-            copy_out = nc.vector.tensor_copy if g == 0 else nc.scalar.copy
+            copy_out = nc.vector.tensor_copy if g == 0 and c >= 2 else nc.scalar.copy
             for half in range(2):
                 xt = banks.tile([P, 2, 2 * P], F32, tag="bank")
                 for jj in range(2):

@@ -18,14 +18,14 @@ BATCH, D_IN, D_OUT = 4096, 1024, 256
 PASSES = D_IN // K_PASS
 GATES = 3
 HALVES = D_OUT // P
-CHUNK = 512
-ROWS = CHUNK // P
-N_CHUNKS = BATCH // CHUNK
+BANK = 512
 WORDS = K_PASS // 2
 BLOCK = 32
 QUADS = P // BLOCK
-ROW_BLOCKS = CHUNK // BLOCK
 RUN = HALVES * BLOCK
+CHUNK_ROWS = [512] * 7 + [256, 256]
+N_CHUNKS = len(CHUNK_ROWS)
+assert sum(CHUNK_ROWS) == BATCH
 
 FLOPS = 2 * BATCH * D_IN * GATES * D_OUT
 
@@ -38,9 +38,7 @@ def tile_lstm_pa_t_kernel(
     gate_scales = [Wxi_scales, Wxc_scales, Wxo_scales]
     gate_biases = [bxi, bxc, bxo]
     gate_funcs = [FUNC.Sigmoid, FUNC.Tanh, FUNC.Sigmoid]
-
-    x_view = x.rearrange("(c j p) k -> c p j k", p=P, j=ROWS)
-    out_view = out.rearrange("(c R r) (F e) -> c F r R e", R=ROW_BLOCKS, r=BLOCK, F=QUADS)
+    first_row = [sum(CHUNK_ROWS[:c]) for c in range(N_CHUNKS)]
 
     with ExitStack() as stack:
         consts = stack.enter_context(tc.tile_pool(name="consts", bufs=1))
@@ -74,13 +72,14 @@ def tile_lstm_pa_t_kernel(
         nc.scalar.activation(out=warm[:, 1:2], in_=warm[:, 0:1], func=FUNC.Sigmoid)
 
         def load_chunk(c):
-            x_sb = x_pool.tile([P, ROWS, D_IN], BF16)
+            rows = CHUNK_ROWS[c] // P
+            x_sb = x_pool.tile([P, rows, D_IN], BF16)
+            x_view = x[first_row[c] : first_row[c] + CHUNK_ROWS[c], :].rearrange("(j p) k -> p j k", p=P)
             pieces = PASSES if c == 0 else 1
             for piece in range(pieces):
                 ks = slice(piece * D_IN // pieces, (piece + 1) * D_IN // pieces)
-                for half in range(2):
-                    js = slice(2 * half, 2 * half + 2)
-                    nc.sync.dma_start(out=x_sb[:, js, ks], in_=x_view[c][:, js, ks])
+                for j0 in range(0, rows, 2):
+                    nc.sync.dma_start(out=x_sb[:, j0 : j0 + 2, ks], in_=x_view[:, j0 : j0 + 2, ks])
             x_tiles[c] = x_sb
 
         w_codes_in = consts.tile([P, GATES, PASSES, D_OUT], U32, align_bytes=64)
@@ -126,38 +125,36 @@ def tile_lstm_pa_t_kernel(
             load_chunk(c)
 
         def transpose_pass(c, g):
-            grouped = grouped_pool.tile([P, PACK * CHUNK], BF16, align_bytes=64)
+            grouped = grouped_pool.tile([P, PACK * CHUNK_ROWS[c]], BF16, align_bytes=64)
             grouped_words = grouped[:].bitcast(F32).rearrange("p (n u) -> p n u", u=2)
             copy_out = nc.vector.tensor_copy if g == 0 and c >= 2 else nc.scalar.copy
-            for half in range(2):
-                xt = banks.tile([P, 2, 2 * P], F32, tag="bank")
-                for jj in range(2):
-                    row_words = x_tiles[c][:, 2 * half + jj, :].bitcast(F32)
+            for n0 in range(0, CHUNK_ROWS[c], BANK // 2):
+                width = min(BANK // 2, CHUNK_ROWS[c] - n0)
+                xt = banks.tile([P, 2, width], F32, tag="bank")
+                for n1 in range(0, width, P):
+                    row_words = x_tiles[c][:, (n0 + n1) // P, :].bitcast(F32)
                     for u in range(2):
                         nc.tensor.transpose(
-                            out=xt[:, u, jj * P : (jj + 1) * P],
+                            out=xt[:, u, n1 : n1 + P],
                             in_=row_words[:, WORDS * g + u : WORDS * (g + 1) : 2],
                             identity=ident[:],
                         )
-                copy_out(
-                    out=grouped_words[:, 2 * P * half : 2 * P * (half + 1), :],
-                    in_=xt[:].rearrange("p u n -> p n u"),
-                )
+                copy_out(out=grouped_words[:, n0 : n0 + width, :], in_=xt[:].rearrange("p u n -> p n u"))
             grouped_tiles[(c, g)] = grouped
 
         def quantise_pass(c, g):
-            x_codes = operand_pool.tile([P, CHUNK], U32, align_bytes=64)
-            x_plane = operand_pool.tile([P, CHUNK], U8, align_bytes=64)
+            x_codes = operand_pool.tile([P, CHUNK_ROWS[c]], U32, align_bytes=64)
+            x_plane = operand_pool.tile([P, CHUNK_ROWS[c]], U8, align_bytes=64)
             nc.vector.quantize_mx(out=x_codes[:].bitcast(FP8X4), scales=x_plane[:], in_=grouped_tiles[(c, g)][:])
             code_tiles[(c, g)] = x_codes
             plane_tiles[(c, g)] = x_plane
 
         def gate_half(c, gate, h):
             if h == 0:
-                gate_sb = gate_pool.tile([P, HALVES, CHUNK], F32, tag="gate%d" % gate)
+                gate_sb = gate_pool.tile([P, HALVES, CHUNK_ROWS[c]], F32, tag="gate%d" % gate)
                 gate_tiles[(c, gate)] = gate_sb
             feats = slice(h * P, (h + 1) * P)
-            acc = banks.tile([P, CHUNK], F32, tag="bank")
+            acc = banks.tile([P, CHUNK_ROWS[c]], F32, tag="bank")
             for g in range(PASSES):
                 nc.tensor.matmul_mx(
                     out=acc[:],
@@ -179,7 +176,7 @@ def tile_lstm_pa_t_kernel(
 
         def state_product(c, h):
             if h == 0:
-                state = gate_pool.tile([P, HALVES, CHUNK], F32)
+                state = gate_pool.tile([P, HALVES, CHUNK_ROWS[c]], F32)
                 state_tiles[c] = state
             nc.vector.tensor_mul(
                 out=state_tiles[c][:, h, :], in0=gate_tiles[(c, 1)][:, h, :], in1=gate_tiles[(c, 0)][:, h, :]
@@ -187,13 +184,13 @@ def tile_lstm_pa_t_kernel(
 
         def tanh_state(c, h):
             if h == 0:
-                tanh_sb = gate_pool.tile([P, HALVES, CHUNK], F32)
+                tanh_sb = gate_pool.tile([P, HALVES, CHUNK_ROWS[c]], F32)
                 tanh_tiles[c] = tanh_sb
             nc.scalar.activation(out=tanh_tiles[c][:, h, :], in_=state_tiles[c][:, h, :], func=FUNC.Tanh)
 
         def output_product(c, h):
             if h == 0:
-                result = gate_pool.tile([P, ROW_BLOCKS, HALVES, BLOCK], F32, align_bytes=64)
+                result = gate_pool.tile([P, CHUNK_ROWS[c] // BLOCK, HALVES, BLOCK], F32, align_bytes=64)
                 result_tiles[c] = result
             nc.vector.tensor_mul(
                 out=result_tiles[c][:, :, h, :],
@@ -202,18 +199,21 @@ def tile_lstm_pa_t_kernel(
             )
 
         def transpose_out(c):
-            out_sb = out_pool.tile([P, ROW_BLOCKS * RUN], F32, align_bytes=64)
+            out_sb = out_pool.tile([P, HALVES * CHUNK_ROWS[c]], F32, align_bytes=64)
             nc.vector.transpose(out=out_sb[:], in_=result_tiles[c][:].rearrange("p R h r -> p (R h r)"))
+            out_view = out[first_row[c] : first_row[c] + CHUNK_ROWS[c], :].rearrange(
+                "(R r) (F e) -> F r R e", r=BLOCK, F=QUADS
+            )
             for quad in range(QUADS):
                 nc.sync.dma_start(
-                    out=out_view[c][quad],
+                    out=out_view[quad],
                     in_=out_sb[quad * BLOCK : (quad + 1) * BLOCK, :].rearrange("r (R e) -> r R e", e=RUN),
                 )
 
         for g in range(PASSES):
             transpose_pass(0, g)
 
-        bias_bank = banks.tile([P, CHUNK], F32, tag="bank")
+        bias_bank = banks.tile([P, BANK], F32, tag="bank")
         nc.tensor.transpose(out=bias_bank[:, 0:P], in_=bias_rows_f32[:], identity=ident[:])
         bias_cols = consts.tile([P, GATES * HALVES], F32)
         nc.vector.tensor_copy(out=bias_cols[:], in_=bias_bank[:, 0 : GATES * HALVES])

@@ -43,8 +43,8 @@ def tile_lstm_pa_t_kernel(
     with ExitStack() as stack:
         consts = stack.enter_context(tc.tile_pool(name="consts", bufs=1))
         x_pool = stack.enter_context(tc.tile_pool(name="x", bufs=N_CHUNKS))
-        grouped_pool = stack.enter_context(tc.tile_pool(name="grouped", bufs=4))
-        operand_pool = stack.enter_context(tc.tile_pool(name="operand", bufs=4))
+        grouped_pool = stack.enter_context(tc.tile_pool(name="grouped", bufs=2))
+        operand_pool = stack.enter_context(tc.tile_pool(name="operand", bufs=2))
         gate_pool = stack.enter_context(tc.tile_pool(name="gate", bufs=3))
         out_pool = stack.enter_context(tc.tile_pool(name="out", bufs=3))
         banks = stack.enter_context(tc.psum_pool(name="banks", bufs=8))
@@ -125,8 +125,10 @@ def tile_lstm_pa_t_kernel(
             load_chunk(c)
 
         def transpose_pass(c, g):
-            grouped = grouped_pool.tile([P, PACK * CHUNK_ROWS[c]], BF16, align_bytes=64)
-            grouped_words = grouped[:].bitcast(F32).rearrange("p (n u) -> p n u", u=2)
+            if g == 0:
+                grouped = grouped_pool.tile([P, PASSES, PACK * CHUNK_ROWS[c]], BF16, align_bytes=64)
+                grouped_tiles[c] = grouped
+            grouped_words = grouped_tiles[c][:, g, :].bitcast(F32).rearrange("p (n u) -> p n u", u=2)
             copy_out = nc.vector.tensor_copy if g == 0 and c >= 2 else nc.scalar.copy
             for n0 in range(0, CHUNK_ROWS[c], BANK // 2):
                 width = min(BANK // 2, CHUNK_ROWS[c] - n0)
@@ -140,14 +142,15 @@ def tile_lstm_pa_t_kernel(
                             identity=ident[:],
                         )
                 copy_out(out=grouped_words[:, n0 : n0 + width, :], in_=xt[:].rearrange("p u n -> p n u"))
-            grouped_tiles[(c, g)] = grouped
 
-        def quantise_pass(c, g):
-            x_codes = operand_pool.tile([P, CHUNK_ROWS[c]], U32, align_bytes=64)
-            x_plane = operand_pool.tile([P, CHUNK_ROWS[c]], U8, align_bytes=64)
-            nc.vector.quantize_mx(out=x_codes[:].bitcast(FP8X4), scales=x_plane[:], in_=grouped_tiles[(c, g)][:])
-            code_tiles[(c, g)] = x_codes
-            plane_tiles[(c, g)] = x_plane
+        def quantise_chunk(c):
+            x_codes = operand_pool.tile([P, PASSES * CHUNK_ROWS[c]], U32, align_bytes=64)
+            x_plane = operand_pool.tile([P, PASSES * CHUNK_ROWS[c]], U8, align_bytes=64)
+            nc.vector.quantize_mx(
+                out=x_codes[:].bitcast(FP8X4), scales=x_plane[:], in_=grouped_tiles[c][:].rearrange("p g n -> p (g n)")
+            )
+            code_tiles[c] = x_codes
+            plane_tiles[c] = x_plane
 
         def gate_half(c, gate, h):
             if h == 0:
@@ -156,12 +159,13 @@ def tile_lstm_pa_t_kernel(
             feats = slice(h * P, (h + 1) * P)
             acc = banks.tile([P, CHUNK_ROWS[c]], F32, tag="bank")
             for g in range(PASSES):
+                cols = slice(g * CHUNK_ROWS[c], (g + 1) * CHUNK_ROWS[c])
                 nc.tensor.matmul_mx(
                     out=acc[:],
                     lhsT=w_codes[:, gate, g, feats].bitcast(FP8X4),
                     lhsT_scale=w_planes[:, gate, g * D_OUT + h * P : g * D_OUT + (h + 1) * P],
-                    rhs=code_tiles[(c, g)][:].bitcast(FP8X4),
-                    rhs_scale=plane_tiles[(c, g)][:],
+                    rhs=code_tiles[c][:, cols].bitcast(FP8X4),
+                    rhs_scale=plane_tiles[c][:, cols],
                     start=(g == 0),
                     stop=(g == PASSES - 1),
                 )
@@ -218,8 +222,7 @@ def tile_lstm_pa_t_kernel(
         bias_cols = consts.tile([P, GATES * HALVES], F32)
         nc.vector.tensor_copy(out=bias_cols[:], in_=bias_bank[:, 0 : GATES * HALVES])
 
-        for g in range(PASSES):
-            quantise_pass(0, g)
+        quantise_chunk(0)
 
         for c in range(N_CHUNKS + 2):
             if 1 <= c <= N_CHUNKS:
@@ -233,11 +236,12 @@ def tile_lstm_pa_t_kernel(
                     permute_weight(gate)
             if c >= 2:
                 transpose_out(c - 2)
-            for half in range(2):
-                if 1 <= c <= N_CHUNKS:
-                    output_product(c - 1, half)
-                if c + 1 < N_CHUNKS:
-                    quantise_pass(c + 1, half)
+            if 1 <= c <= N_CHUNKS:
+                output_product(c - 1, 0)
+            if c + 1 < N_CHUNKS:
+                quantise_chunk(c + 1)
+            if 1 <= c <= N_CHUNKS:
+                output_product(c - 1, 1)
             if c < N_CHUNKS:
                 for h in range(HALVES):
                     gate_half(c, 0, h)

@@ -76,9 +76,9 @@ def tile_lstm_pa_t_kernel(
             x_sb = x_pool.tile([P, rows, D_IN], BF16)
             x_view = x[first_row[c] : first_row[c] + CHUNK_ROWS[c], :].rearrange("(j p) k -> p j k", p=P)
             pieces = PASSES if c == 0 else 1
-            for piece in range(pieces):
-                ks = slice(piece * D_IN // pieces, (piece + 1) * D_IN // pieces)
-                for j0 in range(0, rows, 2):
+            for j0 in range(0, rows, 2):
+                for piece in range(pieces):
+                    ks = slice(piece * D_IN // pieces, (piece + 1) * D_IN // pieces)
                     nc.sync.dma_start(out=x_sb[:, j0 : j0 + 2, ks], in_=x_view[:, j0 : j0 + 2, ks])
             x_tiles[c] = x_sb
 
@@ -124,24 +124,24 @@ def tile_lstm_pa_t_kernel(
         for c in range(2, N_CHUNKS):
             load_chunk(c)
 
-        def transpose_pass(c, g):
-            if g == 0:
-                grouped = grouped_pool.tile([P, PASSES, PACK * CHUNK_ROWS[c]], BF16, align_bytes=64)
-                grouped_tiles[c] = grouped
-            grouped_words = grouped_tiles[c][:, g, :].bitcast(F32).rearrange("p (n u) -> p n u", u=2)
-            copy_out = nc.vector.tensor_copy if g == 0 and c >= 2 else nc.scalar.copy
+        def transpose_chunk(c):
+            grouped = grouped_pool.tile([P, PASSES, PACK * CHUNK_ROWS[c]], BF16, align_bytes=64)
+            grouped_tiles[c] = grouped
             for n0 in range(0, CHUNK_ROWS[c], BANK // 2):
                 width = min(BANK // 2, CHUNK_ROWS[c] - n0)
-                xt = banks.tile([P, 2, width], F32, tag="bank")
-                for n1 in range(0, width, P):
-                    row_words = x_tiles[c][:, (n0 + n1) // P, :].bitcast(F32)
-                    for u in range(2):
-                        nc.tensor.transpose(
-                            out=xt[:, u, n1 : n1 + P],
-                            in_=row_words[:, WORDS * g + u : WORDS * (g + 1) : 2],
-                            identity=ident[:],
-                        )
-                copy_out(out=grouped_words[:, n0 : n0 + width, :], in_=xt[:].rearrange("p u n -> p n u"))
+                for g in range(PASSES):
+                    grouped_words = grouped[:, g, :].bitcast(F32).rearrange("p (n u) -> p n u", u=2)
+                    copy_out = nc.vector.tensor_copy if g == 0 and c >= 2 else nc.scalar.copy
+                    xt = banks.tile([P, 2, width], F32, tag="bank")
+                    for n1 in range(0, width, P):
+                        row_words = x_tiles[c][:, (n0 + n1) // P, :].bitcast(F32)
+                        for u in range(2):
+                            nc.tensor.transpose(
+                                out=xt[:, u, n1 : n1 + P],
+                                in_=row_words[:, WORDS * g + u : WORDS * (g + 1) : 2],
+                                identity=ident[:],
+                            )
+                    copy_out(out=grouped_words[:, n0 : n0 + width, :], in_=xt[:].rearrange("p u n -> p n u"))
 
         def quantise_chunk(c):
             x_codes = operand_pool.tile([P, PASSES * CHUNK_ROWS[c]], U32, align_bytes=64)
@@ -214,8 +214,7 @@ def tile_lstm_pa_t_kernel(
                     in_=out_sb[quad * BLOCK : (quad + 1) * BLOCK, :].rearrange("r (R e) -> r R e", e=RUN),
                 )
 
-        for g in range(PASSES):
-            transpose_pass(0, g)
+        transpose_chunk(0)
 
         bias_bank = banks.tile([P, BANK], F32, tag="bank")
         nc.tensor.transpose(out=bias_bank[:, 0:P], in_=bias_rows_f32[:], identity=ident[:])
@@ -229,8 +228,7 @@ def tile_lstm_pa_t_kernel(
                 for h in range(HALVES):
                     tanh_state(c - 1, h)
             if c + 1 < N_CHUNKS:
-                for g in range(PASSES):
-                    transpose_pass(c + 1, g)
+                transpose_chunk(c + 1)
             if c == 0:
                 for gate in range(GATES):
                     permute_weight(gate)

@@ -53,6 +53,14 @@ def tile_lstm_pa_t_kernel(
         x_tiles, grouped_tiles, code_tiles, plane_tiles = {}, {}, {}, {}
         gate_tiles, state_tiles, tanh_tiles, result_tiles = {}, {}, {}, {}
 
+        idle_lhs = consts.tile([P, P], BF16)
+        idle_rhs = consts.tile([P, BANK], BF16)
+        nc.vector.memset(idle_lhs[:], 0.0)
+        nc.vector.memset(idle_rhs[:], 0.0)
+        idle_bank = banks.tile([P, BANK], F32, tag="bank")
+        for i in range(5):
+            nc.tensor.matmul(out=idle_bank[:], lhsT=idle_lhs[:], rhs=idle_rhs[:], start=True, stop=True)
+
         ident = consts.tile([P, P], F32)
         make_identity(nc, ident[:])
 
@@ -75,11 +83,9 @@ def tile_lstm_pa_t_kernel(
             rows = CHUNK_ROWS[c] // P
             x_sb = x_pool.tile([P, rows, D_IN], BF16)
             x_view = x[first_row[c] : first_row[c] + CHUNK_ROWS[c], :].rearrange("(j p) k -> p j k", p=P)
-            pieces = PASSES if c == 0 else 1
-            for j0 in range(0, rows, 2):
-                for piece in range(pieces):
-                    ks = slice(piece * D_IN // pieces, (piece + 1) * D_IN // pieces)
-                    nc.sync.dma_start(out=x_sb[:, j0 : j0 + 2, ks], in_=x_view[:, j0 : j0 + 2, ks])
+            step = 1 if c == 0 else 2
+            for j0 in range(0, rows, step):
+                nc.sync.dma_start(out=x_sb[:, j0 : j0 + step, :], in_=x_view[:, j0 : j0 + step, :])
             x_tiles[c] = x_sb
 
         w_codes_in = consts.tile([P, GATES, PASSES, D_OUT], U32, align_bytes=64)
@@ -131,7 +137,7 @@ def tile_lstm_pa_t_kernel(
                 width = min(BANK // 2, CHUNK_ROWS[c] - n0)
                 for g in range(PASSES):
                     grouped_words = grouped[:, g, :].bitcast(F32).rearrange("p (n u) -> p n u", u=2)
-                    copy_out = nc.vector.tensor_copy if g == 0 and c >= 2 else nc.scalar.copy
+                    copy_out = nc.vector.tensor_copy if g == 0 and c != 1 else nc.scalar.copy
                     xt = banks.tile([P, 2, width], F32, tag="bank")
                     for n1 in range(0, width, P):
                         row_words = x_tiles[c][:, (n0 + n1) // P, :].bitcast(F32)

@@ -130,24 +130,26 @@ def tile_lstm_pa_t_kernel(
         for c in range(2, N_CHUNKS):
             load_chunk(c)
 
-        def transpose_chunk(c):
-            grouped = grouped_pool.tile([P, PASSES, PACK * CHUNK_ROWS[c]], BF16, align_bytes=64)
-            grouped_tiles[c] = grouped
-            for n0 in range(0, CHUNK_ROWS[c], BANK // 2):
-                width = min(BANK // 2, CHUNK_ROWS[c] - n0)
-                for g in range(PASSES):
-                    grouped_words = grouped[:, g, :].bitcast(F32).rearrange("p (n u) -> p n u", u=2)
-                    copy_out = nc.vector.tensor_copy if g == 0 and c != 1 else nc.scalar.copy
-                    xt = banks.tile([P, 2, width], F32, tag="bank")
-                    for n1 in range(0, width, P):
-                        row_words = x_tiles[c][:, (n0 + n1) // P, :].bitcast(F32)
-                        for u in range(2):
-                            nc.tensor.transpose(
-                                out=xt[:, u, n1 : n1 + P],
-                                in_=row_words[:, WORDS * g + u : WORDS * (g + 1) : 2],
-                                identity=ident[:],
-                            )
-                    copy_out(out=grouped_words[:, n0 : n0 + width, :], in_=xt[:].rearrange("p u n -> p n u"))
+        def transpose_bank(c, n0, g):
+            if n0 == 0 and g == 0:
+                grouped = grouped_pool.tile([P, PASSES, PACK * CHUNK_ROWS[c]], BF16, align_bytes=64)
+                grouped_tiles[c] = grouped
+            width = BANK // 2
+            grouped_words = grouped_tiles[c][:, g, :].bitcast(F32).rearrange("p (n u) -> p n u", u=2)
+            copy_out = nc.vector.tensor_copy if g == 0 and c != 1 else nc.scalar.copy
+            xt = banks.tile([P, 2, width], F32, tag="bank")
+            for n1 in range(0, width, P):
+                row_words = x_tiles[c][:, (n0 + n1) // P, :].bitcast(F32)
+                for u in range(2):
+                    nc.tensor.transpose(
+                        out=xt[:, u, n1 : n1 + P],
+                        in_=row_words[:, WORDS * g + u : WORDS * (g + 1) : 2],
+                        identity=ident[:],
+                    )
+            copy_out(out=grouped_words[:, n0 : n0 + width, :], in_=xt[:].rearrange("p u n -> p n u"))
+
+        def x_banks(c):
+            return [(n0, g) for n0 in range(0, CHUNK_ROWS[c], BANK // 2) for g in range(PASSES)]
 
         def quantise_chunk(c):
             x_codes = operand_pool.tile([P, PASSES * CHUNK_ROWS[c]], U32, align_bytes=64)
@@ -185,18 +187,19 @@ def tile_lstm_pa_t_kernel(
             )
 
         def state_product(c, h):
+            on_gpsimd = h == 1 and CHUNK_ROWS[c] == BANK
             if h == 0:
                 state = gate_pool.tile([P, HALVES, CHUNK_ROWS[c]], F32)
-                state_tiles[c] = state
-            nc.vector.tensor_mul(
-                out=state_tiles[c][:, h, :], in0=gate_tiles[(c, 1)][:, h, :], in1=gate_tiles[(c, 0)][:, h, :]
-            )
+                state_tiles[c, 0] = state[:, 0, :]
+                state_tiles[c, 1] = gate_tiles[(c, 0)][:, 0, :] if CHUNK_ROWS[c] == BANK else state[:, 1, :]
+            multiply = nc.gpsimd.tensor_mul if on_gpsimd else nc.vector.tensor_mul
+            multiply(out=state_tiles[c, h], in0=gate_tiles[(c, 1)][:, h, :], in1=gate_tiles[(c, 0)][:, h, :])
 
         def tanh_state(c, h):
             if h == 0:
                 tanh_sb = gate_pool.tile([P, HALVES, CHUNK_ROWS[c]], F32)
                 tanh_tiles[c] = tanh_sb
-            nc.scalar.activation(out=tanh_tiles[c][:, h, :], in_=state_tiles[c][:, h, :], func=FUNC.Tanh)
+            nc.scalar.activation(out=tanh_tiles[c][:, h, :], in_=state_tiles[c, h], func=FUNC.Tanh)
 
         def output_product(c, h):
             if h == 0:
@@ -220,7 +223,8 @@ def tile_lstm_pa_t_kernel(
                     in_=out_sb[quad * BLOCK : (quad + 1) * BLOCK, :].rearrange("r (R e) -> r R e", e=RUN),
                 )
 
-        transpose_chunk(0)
+        for n0, g in x_banks(0):
+            transpose_bank(0, n0, g)
 
         bias_bank = banks.tile([P, BANK], F32, tag="bank")
         nc.tensor.transpose(out=bias_bank[:, 0:P], in_=bias_rows_f32[:], identity=ident[:])
@@ -231,10 +235,15 @@ def tile_lstm_pa_t_kernel(
 
         for c in range(N_CHUNKS + 2):
             if 1 <= c <= N_CHUNKS:
-                for h in range(HALVES):
-                    tanh_state(c - 1, h)
+                tanh_state(c - 1, 0)
             if c + 1 < N_CHUNKS:
-                transpose_chunk(c + 1)
+                for n0, g in x_banks(c + 1)[:2]:
+                    transpose_bank(c + 1, n0, g)
+            if 1 <= c <= N_CHUNKS:
+                tanh_state(c - 1, 1)
+            if c + 1 < N_CHUNKS:
+                for n0, g in x_banks(c + 1)[2:]:
+                    transpose_bank(c + 1, n0, g)
             if c == 0:
                 for gate in range(GATES):
                     permute_weight(gate)

@@ -136,7 +136,8 @@ def tile_lstm_pa_t_kernel(
                 grouped_tiles[c] = grouped
             width = BANK // 2
             grouped_words = grouped_tiles[c][:, g, :].bitcast(F32).rearrange("p (n u) -> p n u", u=2)
-            copy_out = nc.vector.tensor_copy if g == 0 and c != 1 else nc.scalar.copy
+            on_vector = (n0, g) != x_banks(c)[-1] if c >= 2 else g == 0 and c == 0
+            copy_out = nc.vector.tensor_copy if on_vector else nc.scalar.copy
             xt = banks.tile([P, 2, width], F32, tag="bank")
             for n1 in range(0, width, P):
                 row_words = x_tiles[c][:, (n0 + n1) // P, :].bitcast(F32)
@@ -237,12 +238,7 @@ def tile_lstm_pa_t_kernel(
             if 1 <= c <= N_CHUNKS:
                 tanh_state(c - 1, 0)
             if c + 1 < N_CHUNKS:
-                for n0, g in x_banks(c + 1)[:2]:
-                    transpose_bank(c + 1, n0, g)
-            if 1 <= c <= N_CHUNKS:
-                tanh_state(c - 1, 1)
-            if c + 1 < N_CHUNKS:
-                for n0, g in x_banks(c + 1)[2:]:
+                for n0, g in x_banks(c + 1):
                     transpose_bank(c + 1, n0, g)
             if c == 0:
                 for gate in range(GATES):
@@ -253,12 +249,16 @@ def tile_lstm_pa_t_kernel(
                 output_product(c - 1, 0)
             if c + 1 < N_CHUNKS:
                 quantise_chunk(c + 1)
+            if c < N_CHUNKS:
+                gate_half(c, 0, 0)
             if 1 <= c <= N_CHUNKS:
+                tanh_state(c - 1, 1)
                 output_product(c - 1, 1)
             if c < N_CHUNKS:
-                for h in range(HALVES):
-                    gate_half(c, 0, h)
-                    gate_half(c, 1, h)
-                    state_product(c, h)
+                gate_half(c, 1, 0)
+                state_product(c, 0)
+                gate_half(c, 0, 1)
+                gate_half(c, 1, 1)
+                state_product(c, 1)
                 for h in range(HALVES):
                     gate_half(c, 2, h)

@@ -25,6 +25,8 @@ QUADS = P // BLOCK
 RUN = HALVES * BLOCK
 CHUNK_ROWS = [512] * 7 + [256, 256]
 N_CHUNKS = len(CHUNK_ROWS)
+LAST_ROWS = CHUNK_ROWS[-1]
+FIRST_TURNED = N_CHUNKS - 2
 assert sum(CHUNK_ROWS) == BATCH
 
 FLOPS = 2 * BATCH * D_IN * GATES * D_OUT
@@ -47,6 +49,7 @@ def tile_lstm_pa_t_kernel(
         operand_pool = stack.enter_context(tc.tile_pool(name="operand", bufs=2))
         gate_pool = stack.enter_context(tc.tile_pool(name="gate", bufs=3))
         out_pool = stack.enter_context(tc.tile_pool(name="out", bufs=3))
+        turned_pool = stack.enter_context(tc.tile_pool(name="turned", bufs=2))
         banks = stack.enter_context(tc.psum_pool(name="banks", bufs=8))
         stack.enter_context(tc.manual_schedule())
 
@@ -224,6 +227,26 @@ def tile_lstm_pa_t_kernel(
                     in_=out_sb[quad * BLOCK : (quad + 1) * BLOCK, :].rearrange("r (R e) -> r R e", e=RUN),
                 )
 
+        def turn(features):
+            bank = banks.tile([P, LAST_ROWS // P, P], F32, tag="bank")
+            for j in range(LAST_ROWS // P):
+                nc.tensor.transpose(out=bank[:, j, :], in_=features[:, j * P : (j + 1) * P], identity=ident[:])
+            return bank
+
+        def finish_turned(c, state_banks, gate_banks):
+            tanh_sb = turned_pool.tile([P, HALVES, LAST_ROWS // P, P], F32)
+            out_sb = turned_pool.tile([P, LAST_ROWS // P, D_OUT], F32)
+            for h in range(HALVES):
+                nc.scalar.activation(out=tanh_sb[:, h, :, :], in_=state_banks[h][:], func=FUNC.Tanh)
+                nc.vector.tensor_mul(
+                    out=out_sb[:].rearrange("p j (F h f) -> p h j F f", F=QUADS, h=HALVES)[:, h],
+                    in0=tanh_sb[:, h, :, :].rearrange("p j (F f) -> p j F f", F=QUADS),
+                    in1=gate_banks[h][:].rearrange("p j (F f) -> p j F f", F=QUADS),
+                )
+            nc.sync.dma_start(
+                out=out[first_row[c] : first_row[c] + LAST_ROWS, :].rearrange("(j p) e -> p j e", p=P), in_=out_sb[:]
+            )
+
         for n0, g in x_banks(0):
             transpose_bank(0, n0, g)
 
@@ -234,8 +257,8 @@ def tile_lstm_pa_t_kernel(
 
         quantise_chunk(0)
 
-        for c in range(N_CHUNKS + 2):
-            if 1 <= c <= N_CHUNKS:
+        for c in range(N_CHUNKS):
+            if 1 <= c < FIRST_TURNED + 1:
                 tanh_state(c - 1, 0)
             if c + 1 < N_CHUNKS:
                 for n0, g in x_banks(c + 1):
@@ -245,20 +268,23 @@ def tile_lstm_pa_t_kernel(
                     permute_weight(gate)
             if c >= 2:
                 transpose_out(c - 2)
-            if 1 <= c <= N_CHUNKS:
+            if 1 <= c < FIRST_TURNED + 1:
                 output_product(c - 1, 0)
             if c + 1 < N_CHUNKS:
                 quantise_chunk(c + 1)
-            if c < N_CHUNKS:
-                gate_half(c, 0, 0)
-            if 1 <= c <= N_CHUNKS:
+            gate_half(c, 0, 0)
+            if 1 <= c < FIRST_TURNED + 1:
                 tanh_state(c - 1, 1)
                 output_product(c - 1, 1)
-            if c < N_CHUNKS:
-                gate_half(c, 1, 0)
-                state_product(c, 0)
-                gate_half(c, 0, 1)
-                gate_half(c, 1, 1)
-                state_product(c, 1)
-                for h in range(HALVES):
-                    gate_half(c, 2, h)
+            gate_half(c, 1, 0)
+            state_product(c, 0)
+            gate_half(c, 0, 1)
+            gate_half(c, 1, 1)
+            state_product(c, 1)
+            for h in range(HALVES):
+                gate_half(c, 2, h)
+
+        for c in range(FIRST_TURNED, N_CHUNKS):
+            state_banks = [turn(state_tiles[c, h]) for h in range(HALVES)]
+            gate_banks = [turn(gate_tiles[(c, 2)][:, h, :]) for h in range(HALVES)]
+            finish_turned(c, state_banks, gate_banks)

@@ -61,7 +61,7 @@ def tile_lstm_pa_t_kernel(
         nc.vector.memset(idle_lhs[:], 0.0)
         nc.vector.memset(idle_rhs[:], 0.0)
         idle_bank = banks.tile([P, BANK], F32, tag="bank")
-        for i in range(5):
+        for i in range(4):
             nc.tensor.matmul(out=idle_bank[:], lhsT=idle_lhs[:], rhs=idle_rhs[:], start=True, stop=True)
 
         ident = consts.tile([P, P], F32)
@@ -250,10 +250,7 @@ def tile_lstm_pa_t_kernel(
         for n0, g in x_banks(0):
             transpose_bank(0, n0, g)
 
-        bias_bank = banks.tile([P, BANK], F32, tag="bank")
-        nc.tensor.transpose(out=bias_bank[:, 0:P], in_=bias_rows_f32[:], identity=ident[:])
         bias_cols = consts.tile([P, GATES * HALVES], F32)
-        nc.vector.tensor_copy(out=bias_cols[:], in_=bias_bank[:, 0 : GATES * HALVES])
 
         quantise_chunk(0)
 
@@ -264,8 +261,12 @@ def tile_lstm_pa_t_kernel(
                 for n0, g in x_banks(c + 1):
                     transpose_bank(c + 1, n0, g)
             if c == 0:
-                for gate in range(GATES):
-                    permute_weight(gate)
+                permute_weight(0)
+                bias_bank = banks.tile([P, BANK], F32, tag="bank")
+                nc.tensor.transpose(out=bias_bank[:, 0:P], in_=bias_rows_f32[:], identity=ident[:])
+                nc.vector.tensor_copy(out=bias_cols[:], in_=bias_bank[:, 0 : GATES * HALVES])
+                permute_weight(1)
+                permute_weight(2)
             if c >= 2:
                 transpose_out(c - 2)
             if 1 <= c < FIRST_TURNED + 1:
@@ -276,11 +277,10 @@ def tile_lstm_pa_t_kernel(
             if 1 <= c < FIRST_TURNED + 1:
                 tanh_state(c - 1, 1)
                 output_product(c - 1, 1)
-            gate_half(c, 1, 0)
-            state_product(c, 0)
             gate_half(c, 0, 1)
-            gate_half(c, 1, 1)
-            state_product(c, 1)
+            for h in range(HALVES):
+                gate_half(c, 1, h)
+                state_product(c, h)
             for h in range(HALVES):
                 gate_half(c, 2, h)
 

@@ -92,9 +92,9 @@ def tile_lstm_pa_t_kernel(
             x_tiles[c] = x_sb
 
         w_codes_in = consts.tile([P, GATES, PASSES, D_OUT], U32, align_bytes=64)
-        w_codes = consts.tile([P, GATES, PASSES, D_OUT], U32, align_bytes=64)
+        w_codes = consts.tile([P, GATES, PASSES, D_OUT], U32, align_bytes=256)
         w_planes_in = consts.tile([P, GATES, PASSES * D_OUT], U8, align_bytes=64)
-        w_planes = consts.tile([P, GATES, PASSES * D_OUT], U8, align_bytes=64)
+        w_planes = consts.tile([P, GATES, PASSES * D_OUT], U8, align_bytes=256)
         nc.vector.memset(w_planes_in[:].bitcast(I32), 0)
 
         def load_weight(gate):
@@ -156,8 +156,8 @@ def tile_lstm_pa_t_kernel(
             return [(n0, g) for n0 in range(0, CHUNK_ROWS[c], BANK // 2) for g in range(PASSES)]
 
         def quantise_chunk(c):
-            x_codes = operand_pool.tile([P, PASSES * CHUNK_ROWS[c]], U32, align_bytes=64)
-            x_plane = operand_pool.tile([P, PASSES * CHUNK_ROWS[c]], U8, align_bytes=64)
+            x_codes = operand_pool.tile([P, PASSES * CHUNK_ROWS[c]], U32, align_bytes=256)
+            x_plane = operand_pool.tile([P, PASSES * CHUNK_ROWS[c]], U8, align_bytes=256)
             nc.vector.quantize_mx(
                 out=x_codes[:].bitcast(FP8X4), scales=x_plane[:], in_=grouped_tiles[c][:].rearrange("p g n -> p (g n)")
             )
@@ -236,16 +236,18 @@ def tile_lstm_pa_t_kernel(
         def finish_turned(c, state_banks, gate_banks):
             tanh_sb = turned_pool.tile([P, HALVES, LAST_ROWS // P, P], F32)
             out_sb = turned_pool.tile([P, LAST_ROWS // P, D_OUT], F32)
+            row_blocks = range(LAST_ROWS // P)
             for h in range(HALVES):
                 nc.scalar.activation(out=tanh_sb[:, h, :, :], in_=state_banks[h][:], func=FUNC.Tanh)
-                nc.vector.tensor_mul(
-                    out=out_sb[:].rearrange("p j (F h f) -> p h j F f", F=QUADS, h=HALVES)[:, h],
-                    in0=tanh_sb[:, h, :, :].rearrange("p j (F f) -> p j F f", F=QUADS),
-                    in1=gate_banks[h][:].rearrange("p j (F f) -> p j F f", F=QUADS),
-                )
-            nc.sync.dma_start(
-                out=out[first_row[c] : first_row[c] + LAST_ROWS, :].rearrange("(j p) e -> p j e", p=P), in_=out_sb[:]
-            )
+                for blocks in [slice(0, len(row_blocks))] if h == 0 else [slice(j, j + 1) for j in row_blocks]:
+                    nc.vector.tensor_mul(
+                        out=out_sb[:, blocks, :].rearrange("p j (F h f) -> p h j F f", F=QUADS, h=HALVES)[:, h],
+                        in0=tanh_sb[:, h, blocks, :].rearrange("p j (F f) -> p j F f", F=QUADS),
+                        in1=gate_banks[h][:, blocks, :].rearrange("p j (F f) -> p j F f", F=QUADS),
+                    )
+            out_view = out[first_row[c] : first_row[c] + LAST_ROWS, :].rearrange("(j p) e -> p j e", p=P)
+            for j in row_blocks:
+                nc.sync.dma_start(out=out_view[:, j, :], in_=out_sb[:, j, :])
 
         for n0, g in x_banks(0):
             transpose_bank(0, n0, g)
@@ -257,6 +259,8 @@ def tile_lstm_pa_t_kernel(
         for c in range(N_CHUNKS):
             if 1 <= c < FIRST_TURNED + 1:
                 tanh_state(c - 1, 0)
+            if c >= 2:
+                transpose_out(c - 2)
             if c + 1 < N_CHUNKS:
                 for n0, g in x_banks(c + 1):
                     transpose_bank(c + 1, n0, g)
@@ -267,8 +271,6 @@ def tile_lstm_pa_t_kernel(
                 nc.vector.tensor_copy(out=bias_cols[:], in_=bias_bank[:, 0 : GATES * HALVES])
                 permute_weight(1)
                 permute_weight(2)
-            if c >= 2:
-                transpose_out(c - 2)
             if 1 <= c < FIRST_TURNED + 1:
                 output_product(c - 1, 0)
             if c + 1 < N_CHUNKS:

@@ -12,6 +12,7 @@ FP8X4 = mybir.dt.float8_e4m3fn_x4
 FUNC = mybir.ActivationFunctionType
 
 P = 128
+LINE = 256
 PACK = 4
 K_PASS = P * PACK
 BATCH, D_IN, D_OUT = 4096, 1024, 256
@@ -56,18 +57,18 @@ def tile_lstm_pa_t_kernel(
         x_tiles, grouped_tiles, code_tiles, plane_tiles = {}, {}, {}, {}
         gate_tiles, state_tiles, tanh_tiles, result_tiles = {}, {}, {}, {}
 
-        idle_lhs = consts.tile([P, P], BF16)
-        idle_rhs = consts.tile([P, BANK], BF16)
+        idle_lhs = consts.tile([P, P], BF16, align_bytes=LINE)
+        idle_rhs = consts.tile([P, BANK], BF16, align_bytes=LINE)
         nc.vector.memset(idle_lhs[:], 0.0)
         nc.vector.memset(idle_rhs[:], 0.0)
         idle_bank = banks.tile([P, BANK], F32, tag="bank")
         for i in range(4):
             nc.tensor.matmul(out=idle_bank[:], lhsT=idle_lhs[:], rhs=idle_rhs[:], start=True, stop=True)
 
-        ident = consts.tile([P, P], F32)
+        ident = consts.tile([P, P], F32, align_bytes=LINE)
         make_identity(nc, ident[:])
 
-        bias_rows = consts.tile([P, P], BF16)
+        bias_rows = consts.tile([P, P], BF16, align_bytes=LINE)
         nc.vector.memset(bias_rows[:], 0.0)
         for gate in range(GATES):
             nc.scalar.dma_start(
@@ -75,26 +76,26 @@ def tile_lstm_pa_t_kernel(
                 in_=gate_biases[gate].rearrange("(F h f) -> h F f", F=QUADS, h=HALVES),
             )
 
-        bias_rows_f32 = consts.tile([P, P], F32)
+        bias_rows_f32 = consts.tile([P, P], F32, align_bytes=LINE)
         nc.gpsimd.tensor_copy(out=bias_rows_f32[:], in_=bias_rows[:])
 
-        warm = consts.tile([P, 2], F32)
+        warm = consts.tile([P, 2], F32, align_bytes=LINE)
         nc.vector.memset(warm[:], 0.0)
         nc.scalar.activation(out=warm[:, 1:2], in_=warm[:, 0:1], func=FUNC.Sigmoid)
 
         def load_chunk(c):
             rows = CHUNK_ROWS[c] // P
-            x_sb = x_pool.tile([P, rows, D_IN], BF16)
+            x_sb = x_pool.tile([P, rows, D_IN], BF16, align_bytes=LINE)
             x_view = x[first_row[c] : first_row[c] + CHUNK_ROWS[c], :].rearrange("(j p) k -> p j k", p=P)
             step = 1 if c == 0 else 2
             for j0 in range(0, rows, step):
                 nc.sync.dma_start(out=x_sb[:, j0 : j0 + step, :], in_=x_view[:, j0 : j0 + step, :])
             x_tiles[c] = x_sb
 
-        w_codes_in = consts.tile([P, GATES, PASSES, D_OUT], U32, align_bytes=64)
-        w_codes = consts.tile([P, GATES, PASSES, D_OUT], U32, align_bytes=256)
-        w_planes_in = consts.tile([P, GATES, PASSES * D_OUT], U8, align_bytes=64)
-        w_planes = consts.tile([P, GATES, PASSES * D_OUT], U8, align_bytes=256)
+        w_codes_in = consts.tile([P, GATES, PASSES, D_OUT], U32, align_bytes=LINE)
+        w_codes = consts.tile([P, GATES, PASSES, D_OUT], U32, align_bytes=LINE)
+        w_planes_in = consts.tile([P, GATES, PASSES * D_OUT], U8, align_bytes=LINE)
+        w_planes = consts.tile([P, GATES, PASSES * D_OUT], U8, align_bytes=LINE)
         nc.vector.memset(w_planes_in[:].bitcast(I32), 0)
 
         def load_weight(gate):
@@ -135,7 +136,7 @@ def tile_lstm_pa_t_kernel(
 
         def transpose_bank(c, n0, g):
             if n0 == 0 and g == 0:
-                grouped = grouped_pool.tile([P, PASSES, PACK * CHUNK_ROWS[c]], BF16, align_bytes=64)
+                grouped = grouped_pool.tile([P, PASSES, PACK * CHUNK_ROWS[c]], BF16, align_bytes=LINE)
                 grouped_tiles[c] = grouped
             width = BANK // 2
             grouped_words = grouped_tiles[c][:, g, :].bitcast(F32).rearrange("p (n u) -> p n u", u=2)
@@ -156,8 +157,8 @@ def tile_lstm_pa_t_kernel(
             return [(n0, g) for n0 in range(0, CHUNK_ROWS[c], BANK // 2) for g in range(PASSES)]
 
         def quantise_chunk(c):
-            x_codes = operand_pool.tile([P, PASSES * CHUNK_ROWS[c]], U32, align_bytes=256)
-            x_plane = operand_pool.tile([P, PASSES * CHUNK_ROWS[c]], U8, align_bytes=256)
+            x_codes = operand_pool.tile([P, PASSES * CHUNK_ROWS[c]], U32, align_bytes=LINE)
+            x_plane = operand_pool.tile([P, PASSES * CHUNK_ROWS[c]], U8, align_bytes=LINE)
             nc.vector.quantize_mx(
                 out=x_codes[:].bitcast(FP8X4), scales=x_plane[:], in_=grouped_tiles[c][:].rearrange("p g n -> p (g n)")
             )
@@ -166,7 +167,7 @@ def tile_lstm_pa_t_kernel(
 
         def gate_half(c, gate, h):
             if h == 0:
-                gate_sb = gate_pool.tile([P, HALVES, CHUNK_ROWS[c]], F32, tag="gate%d" % gate)
+                gate_sb = gate_pool.tile([P, HALVES, CHUNK_ROWS[c]], F32, tag="gate%d" % gate, align_bytes=LINE)
                 gate_tiles[(c, gate)] = gate_sb
             feats = slice(h * P, (h + 1) * P)
             acc = banks.tile([P, CHUNK_ROWS[c]], F32, tag="bank")
@@ -193,7 +194,7 @@ def tile_lstm_pa_t_kernel(
         def state_product(c, h):
             on_gpsimd = h == 1 and CHUNK_ROWS[c] == BANK
             if h == 0:
-                state = gate_pool.tile([P, HALVES, CHUNK_ROWS[c]], F32)
+                state = gate_pool.tile([P, HALVES, CHUNK_ROWS[c]], F32, align_bytes=LINE)
                 state_tiles[c, 0] = state[:, 0, :]
                 state_tiles[c, 1] = gate_tiles[(c, 0)][:, 0, :] if CHUNK_ROWS[c] == BANK else state[:, 1, :]
             multiply = nc.gpsimd.tensor_mul if on_gpsimd else nc.vector.tensor_mul
@@ -201,13 +202,13 @@ def tile_lstm_pa_t_kernel(
 
         def tanh_state(c, h):
             if h == 0:
-                tanh_sb = gate_pool.tile([P, HALVES, CHUNK_ROWS[c]], F32)
+                tanh_sb = gate_pool.tile([P, HALVES, CHUNK_ROWS[c]], F32, align_bytes=LINE)
                 tanh_tiles[c] = tanh_sb
             nc.scalar.activation(out=tanh_tiles[c][:, h, :], in_=state_tiles[c, h], func=FUNC.Tanh)
 
         def output_product(c, h):
             if h == 0:
-                result = gate_pool.tile([P, CHUNK_ROWS[c] // BLOCK, HALVES, BLOCK], F32, align_bytes=64)
+                result = gate_pool.tile([P, CHUNK_ROWS[c] // BLOCK, HALVES, BLOCK], F32, align_bytes=LINE)
                 result_tiles[c] = result
             nc.vector.tensor_mul(
                 out=result_tiles[c][:, :, h, :],
@@ -216,7 +217,7 @@ def tile_lstm_pa_t_kernel(
             )
 
         def transpose_out(c):
-            out_sb = out_pool.tile([P, HALVES * CHUNK_ROWS[c]], F32, align_bytes=64)
+            out_sb = out_pool.tile([P, HALVES * CHUNK_ROWS[c]], F32, align_bytes=LINE)
             nc.vector.transpose(out=out_sb[:], in_=result_tiles[c][:].rearrange("p R h r -> p (R h r)"))
             out_view = out[first_row[c] : first_row[c] + CHUNK_ROWS[c], :].rearrange(
                 "(R r) (F e) -> F r R e", r=BLOCK, F=QUADS
@@ -234,8 +235,8 @@ def tile_lstm_pa_t_kernel(
             return bank
 
         def finish_turned(c, state_banks, gate_banks):
-            tanh_sb = turned_pool.tile([P, HALVES, LAST_ROWS // P, P], F32)
-            out_sb = turned_pool.tile([P, LAST_ROWS // P, D_OUT], F32)
+            tanh_sb = turned_pool.tile([P, HALVES, LAST_ROWS // P, P], F32, align_bytes=LINE)
+            out_sb = turned_pool.tile([P, LAST_ROWS // P, D_OUT], F32, align_bytes=LINE)
             row_blocks = range(LAST_ROWS // P)
             for h in range(HALVES):
                 nc.scalar.activation(out=tanh_sb[:, h, :, :], in_=state_banks[h][:], func=FUNC.Tanh)
@@ -252,7 +253,7 @@ def tile_lstm_pa_t_kernel(
         for n0, g in x_banks(0):
             transpose_bank(0, n0, g)
 
-        bias_cols = consts.tile([P, GATES * HALVES], F32)
+        bias_cols = consts.tile([P, GATES * HALVES], F32, align_bytes=LINE)
 
         quantise_chunk(0)
 

from contextlib import ExitStack

import concourse.mybir as mybir
from concourse.masks import make_identity

F32 = mybir.dt.float32
BF16 = mybir.dt.bfloat16
I32 = mybir.dt.int32
U32 = mybir.dt.uint32
U8 = mybir.dt.uint8
FP8X4 = mybir.dt.float8_e4m3fn_x4
FUNC = mybir.ActivationFunctionType

P = 128
LINE = 256
PACK = 4
K_PASS = P * PACK
BATCH, D_IN, D_OUT = 4096, 1024, 256
PASSES = D_IN // K_PASS
GATES = 3
HALVES = D_OUT // P
BANK = 512
WORDS = K_PASS // 2
BLOCK = 32
QUADS = P // BLOCK
RUN = HALVES * BLOCK
CHUNK_ROWS = [512] * 7 + [256, 256]
N_CHUNKS = len(CHUNK_ROWS)
LAST_ROWS = CHUNK_ROWS[-1]
FIRST_TURNED = N_CHUNKS - 2
assert sum(CHUNK_ROWS) == BATCH

FLOPS = 2 * BATCH * D_IN * GATES * D_OUT


def tile_lstm_pa_t_kernel(
    tc, x, Wxi_words, Wxi_scales, bxi, Wxc_words, Wxc_scales, bxc, Wxo_words, Wxo_scales, bxo, out
):
    nc = tc.nc
    gate_words = [Wxi_words, Wxc_words, Wxo_words]
    gate_scales = [Wxi_scales, Wxc_scales, Wxo_scales]
    gate_biases = [bxi, bxc, bxo]
    gate_funcs = [FUNC.Sigmoid, FUNC.Tanh, FUNC.Sigmoid]
    first_row = [sum(CHUNK_ROWS[:c]) for c in range(N_CHUNKS)]

    with ExitStack() as stack:
        consts = stack.enter_context(tc.tile_pool(name="consts", bufs=1))
        x_pool = stack.enter_context(tc.tile_pool(name="x", bufs=N_CHUNKS))
        grouped_pool = stack.enter_context(tc.tile_pool(name="grouped", bufs=2))
        operand_pool = stack.enter_context(tc.tile_pool(name="operand", bufs=2))
        gate_pool = stack.enter_context(tc.tile_pool(name="gate", bufs=3))
        out_pool = stack.enter_context(tc.tile_pool(name="out", bufs=3))
        turned_pool = stack.enter_context(tc.tile_pool(name="turned", bufs=2))
        banks = stack.enter_context(tc.psum_pool(name="banks", bufs=8))
        stack.enter_context(tc.manual_schedule())

        x_tiles, grouped_tiles, code_tiles, plane_tiles = {}, {}, {}, {}
        gate_tiles, state_tiles, tanh_tiles, result_tiles = {}, {}, {}, {}

        idle_lhs = consts.tile([P, P], BF16, align_bytes=LINE)
        idle_rhs = consts.tile([P, BANK], BF16, align_bytes=LINE)
        nc.vector.memset(idle_lhs[:], 0.0)
        nc.vector.memset(idle_rhs[:], 0.0)
        idle_bank = banks.tile([P, BANK], F32, tag="bank")
        for i in range(4):
            nc.tensor.matmul(out=idle_bank[:], lhsT=idle_lhs[:], rhs=idle_rhs[:], start=True, stop=True)

        ident = consts.tile([P, P], F32, align_bytes=LINE)
        make_identity(nc, ident[:])

        bias_rows = consts.tile([P, P], BF16, align_bytes=LINE)
        nc.vector.memset(bias_rows[:], 0.0)
        for gate in range(GATES):
            nc.scalar.dma_start(
                out=bias_rows[HALVES * gate : HALVES * (gate + 1), :].rearrange("h (F f) -> h F f", F=QUADS),
                in_=gate_biases[gate].rearrange("(F h f) -> h F f", F=QUADS, h=HALVES),
            )

        bias_rows_f32 = consts.tile([P, P], F32, align_bytes=LINE)
        nc.gpsimd.tensor_copy(out=bias_rows_f32[:], in_=bias_rows[:])

        warm = consts.tile([P, 2], F32, align_bytes=LINE)
        nc.vector.memset(warm[:], 0.0)
        nc.scalar.activation(out=warm[:, 1:2], in_=warm[:, 0:1], func=FUNC.Sigmoid)

        def load_chunk(c):
            rows = CHUNK_ROWS[c] // P
            x_sb = x_pool.tile([P, rows, D_IN], BF16, align_bytes=LINE)
            x_view = x[first_row[c] : first_row[c] + CHUNK_ROWS[c], :].rearrange("(j p) k -> p j k", p=P)
            step = 1 if c == 0 else 2
            for j0 in range(0, rows, step):
                nc.sync.dma_start(out=x_sb[:, j0 : j0 + step, :], in_=x_view[:, j0 : j0 + step, :])
            x_tiles[c] = x_sb

        w_codes_in = consts.tile([P, GATES, PASSES, D_OUT], U32, align_bytes=LINE)
        w_codes = consts.tile([P, GATES, PASSES, D_OUT], U32, align_bytes=LINE)
        w_planes_in = consts.tile([P, GATES, PASSES * D_OUT], U8, align_bytes=LINE)
        w_planes = consts.tile([P, GATES, PASSES * D_OUT], U8, align_bytes=LINE)
        nc.vector.memset(w_planes_in[:].bitcast(I32), 0)

        def load_weight(gate):
            nc.sync.dma_start(
                out=w_codes_in[:, gate, :, :].bitcast(I32),
                in_=gate_words[gate].rearrange("g p n t -> p g (n t)").bitcast(I32),
            )
            scale_words = gate_scales[gate].bitcast(I32)
            for r in range(4):
                nc.sync.dma_start(
                    out=w_planes_in[r:P:32, gate, :].bitcast(I32).rearrange("q (g n) -> q g n", g=PASSES),
                    in_=scale_words[:, r:16:4, :].rearrange("g q n -> q g n"),
                )

        def permute_weight(gate):
            for h in range(HALVES):
                nc.vector.tensor_copy(
                    out=w_codes[:, gate, :, h * P : (h + 1) * P].bitcast(I32).rearrange("p g (F f) -> p g F f", F=QUADS),
                    in_=w_codes_in[:, gate, :, :].bitcast(I32).rearrange(
                        "p g (F h f) -> p h g F f", F=QUADS, h=HALVES
                    )[:, h],
                )
                nc.vector.tensor_copy(
                    out=w_planes[:, gate, :].bitcast(I32).rearrange(
                        "p (g h F w) -> p h g F w", g=PASSES, h=HALVES, F=QUADS
                    )[:, h],
                    in_=w_planes_in[:, gate, :].bitcast(I32).rearrange(
                        "p (g F h w) -> p h g F w", g=PASSES, h=HALVES, F=QUADS
                    )[:, h],
                )

        load_chunk(0)
        load_chunk(1)
        for gate in range(GATES):
            load_weight(gate)
        for c in range(2, N_CHUNKS):
            load_chunk(c)

        def transpose_bank(c, n0, g):
            if n0 == 0 and g == 0:
                grouped = grouped_pool.tile([P, PASSES, PACK * CHUNK_ROWS[c]], BF16, align_bytes=LINE)
                grouped_tiles[c] = grouped
            width = BANK // 2
            grouped_words = grouped_tiles[c][:, g, :].bitcast(F32).rearrange("p (n u) -> p n u", u=2)
            on_vector = (n0, g) != x_banks(c)[-1] if c >= 2 else g == 0 and c == 0
            copy_out = nc.vector.tensor_copy if on_vector else nc.scalar.copy
            xt = banks.tile([P, 2, width], F32, tag="bank")
            for n1 in range(0, width, P):
                row_words = x_tiles[c][:, (n0 + n1) // P, :].bitcast(F32)
                for u in range(2):
                    nc.tensor.transpose(
                        out=xt[:, u, n1 : n1 + P],
                        in_=row_words[:, WORDS * g + u : WORDS * (g + 1) : 2],
                        identity=ident[:],
                    )
            copy_out(out=grouped_words[:, n0 : n0 + width, :], in_=xt[:].rearrange("p u n -> p n u"))

        def x_banks(c):
            return [(n0, g) for n0 in range(0, CHUNK_ROWS[c], BANK // 2) for g in range(PASSES)]

        def quantise_chunk(c):
            x_codes = operand_pool.tile([P, PASSES * CHUNK_ROWS[c]], U32, align_bytes=LINE)
            x_plane = operand_pool.tile([P, PASSES * CHUNK_ROWS[c]], U8, align_bytes=LINE)
            nc.vector.quantize_mx(
                out=x_codes[:].bitcast(FP8X4), scales=x_plane[:], in_=grouped_tiles[c][:].rearrange("p g n -> p (g n)")
            )
            code_tiles[c] = x_codes
            plane_tiles[c] = x_plane

        def gate_half(c, gate, h):
            if h == 0:
                gate_sb = gate_pool.tile([P, HALVES, CHUNK_ROWS[c]], F32, tag="gate%d" % gate, align_bytes=LINE)
                gate_tiles[(c, gate)] = gate_sb
            feats = slice(h * P, (h + 1) * P)
            acc = banks.tile([P, CHUNK_ROWS[c]], F32, tag="bank")
            for g in range(PASSES):
                cols = slice(g * CHUNK_ROWS[c], (g + 1) * CHUNK_ROWS[c])
                nc.tensor.matmul_mx(
                    out=acc[:],
                    lhsT=w_codes[:, gate, g, feats].bitcast(FP8X4),
                    lhsT_scale=w_planes[:, gate, g * D_OUT + h * P : g * D_OUT + (h + 1) * P],
                    rhs=code_tiles[c][:, cols].bitcast(FP8X4),
                    rhs_scale=plane_tiles[c][:, cols],
                    start=(g == 0),
                    stop=(g == PASSES - 1),
                )
            column = HALVES * gate + h
            nc.scalar.activation(
                out=gate_tiles[(c, gate)][:, h, :],
                in_=acc[:],
                func=gate_funcs[gate],
                bias=bias_cols[:, column : column + 1],
                scale=1.0,
            )

        def state_product(c, h):
            on_gpsimd = h == 1 and CHUNK_ROWS[c] == BANK
            if h == 0:
                state = gate_pool.tile([P, HALVES, CHUNK_ROWS[c]], F32, align_bytes=LINE)
                state_tiles[c, 0] = state[:, 0, :]
                state_tiles[c, 1] = gate_tiles[(c, 0)][:, 0, :] if CHUNK_ROWS[c] == BANK else state[:, 1, :]
            multiply = nc.gpsimd.tensor_mul if on_gpsimd else nc.vector.tensor_mul
            multiply(out=state_tiles[c, h], in0=gate_tiles[(c, 1)][:, h, :], in1=gate_tiles[(c, 0)][:, h, :])

        def tanh_state(c, h):
            if h == 0:
                tanh_sb = gate_pool.tile([P, HALVES, CHUNK_ROWS[c]], F32, align_bytes=LINE)
                tanh_tiles[c] = tanh_sb
            nc.scalar.activation(out=tanh_tiles[c][:, h, :], in_=state_tiles[c, h], func=FUNC.Tanh)

        def output_product(c, h):
            if h == 0:
                result = gate_pool.tile([P, CHUNK_ROWS[c] // BLOCK, HALVES, BLOCK], F32, align_bytes=LINE)
                result_tiles[c] = result
            nc.vector.tensor_mul(
                out=result_tiles[c][:, :, h, :],
                in0=tanh_tiles[c][:, h, :].rearrange("p (R r) -> p R r", r=BLOCK),
                in1=gate_tiles[(c, 2)][:, h, :].rearrange("p (R r) -> p R r", r=BLOCK),
            )

        def transpose_out(c):
            out_sb = out_pool.tile([P, HALVES * CHUNK_ROWS[c]], F32, align_bytes=LINE)
            nc.vector.transpose(out=out_sb[:], in_=result_tiles[c][:].rearrange("p R h r -> p (R h r)"))
            out_view = out[first_row[c] : first_row[c] + CHUNK_ROWS[c], :].rearrange(
                "(R r) (F e) -> F r R e", r=BLOCK, F=QUADS
            )
            for quad in range(QUADS):
                nc.sync.dma_start(
                    out=out_view[quad],
                    in_=out_sb[quad * BLOCK : (quad + 1) * BLOCK, :].rearrange("r (R e) -> r R e", e=RUN),
                )

        def turn(features):
            bank = banks.tile([P, LAST_ROWS // P, P], F32, tag="bank")
            for j in range(LAST_ROWS // P):
                nc.tensor.transpose(out=bank[:, j, :], in_=features[:, j * P : (j + 1) * P], identity=ident[:])
            return bank

        def finish_turned(c, state_banks, gate_banks):
            tanh_sb = turned_pool.tile([P, HALVES, LAST_ROWS // P, P], F32, align_bytes=LINE)
            out_sb = turned_pool.tile([P, LAST_ROWS // P, D_OUT], F32, align_bytes=LINE)
            row_blocks = range(LAST_ROWS // P)
            for h in range(HALVES):
                nc.scalar.activation(out=tanh_sb[:, h, :, :], in_=state_banks[h][:], func=FUNC.Tanh)
                for blocks in [slice(0, len(row_blocks))] if h == 0 else [slice(j, j + 1) for j in row_blocks]:
                    nc.vector.tensor_mul(
                        out=out_sb[:, blocks, :].rearrange("p j (F h f) -> p h j F f", F=QUADS, h=HALVES)[:, h],
                        in0=tanh_sb[:, h, blocks, :].rearrange("p j (F f) -> p j F f", F=QUADS),
                        in1=gate_banks[h][:, blocks, :].rearrange("p j (F f) -> p j F f", F=QUADS),
                    )
            out_view = out[first_row[c] : first_row[c] + LAST_ROWS, :].rearrange("(j p) e -> p j e", p=P)
            for j in row_blocks:
                nc.sync.dma_start(out=out_view[:, j, :], in_=out_sb[:, j, :])

        for n0, g in x_banks(0):
            transpose_bank(0, n0, g)

        bias_cols = consts.tile([P, GATES * HALVES], F32, align_bytes=LINE)

        quantise_chunk(0)

        for c in range(N_CHUNKS):
            if 1 <= c < FIRST_TURNED + 1:
                tanh_state(c - 1, 0)
            if c >= 2:
                transpose_out(c - 2)
            if c + 1 < N_CHUNKS:
                for n0, g in x_banks(c + 1):
                    transpose_bank(c + 1, n0, g)
            if c == 0:
                permute_weight(0)
                bias_bank = banks.tile([P, BANK], F32, tag="bank")
                nc.tensor.transpose(out=bias_bank[:, 0:P], in_=bias_rows_f32[:], identity=ident[:])
                nc.vector.tensor_copy(out=bias_cols[:], in_=bias_bank[:, 0 : GATES * HALVES])
                permute_weight(1)
                permute_weight(2)
            if 1 <= c < FIRST_TURNED + 1:
                output_product(c - 1, 0)
            if c + 1 < N_CHUNKS:
                quantise_chunk(c + 1)
            gate_half(c, 0, 0)
            if 1 <= c < FIRST_TURNED + 1:
                tanh_state(c - 1, 1)
                output_product(c - 1, 1)
            gate_half(c, 0, 1)
            for h in range(HALVES):
                gate_half(c, 1, h)
                state_product(c, h)
            for h in range(HALVES):
                gate_half(c, 2, h)

        for c in range(FIRST_TURNED, N_CHUNKS):
            state_banks = [turn(state_tiles[c, h]) for h in range(HALVES)]
            gate_banks = [turn(gate_tiles[(c, 2)][:, h, :]) for h in range(HALVES)]
            finish_turned(c, state_banks, gate_banks)
